import numpy as np
import ml_dtypes


def mxq(x, axis, fmt="e4m3"):
    dtype, down = {"e4m3": (ml_dtypes.float8_e4m3fn, 7), "e5m2": (ml_dtypes.float8_e5m2, 14)}[fmt]
    v = np.moveaxis(np.asarray(x, np.float32).astype(ml_dtypes.bfloat16).astype(np.float64), axis, -1)
    blocks = v.reshape(v.shape[:-1] + (-1, 32))
    amax = np.abs(blocks).max(-1, keepdims=True)
    byte = np.maximum(np.where(amax > 0, np.frexp(amax)[1] - 1 + 127, 0) - down, 1)
    scale = np.exp2(byte - 127.0)
    codes = (blocks / scale).astype(np.float32).astype(dtype).astype(np.float64)
    return np.moveaxis((codes * scale).reshape(v.shape), -1, axis)


WIDE = False


def mx_kscale(k):
    if not WIDE:
        return np.ones(k)
    levels = np.array([10, -10, 5, -5, 0])
    a = np.random.permutation(np.resize(levels, k // 512 * 4)).reshape(k // 512, 4)
    idx = np.arange(k)
    return np.exp2(a[idx // 512, idx % 128 // 32])


BF16 = ml_dtypes.bfloat16


def bf(x):
    return np.asarray(x, np.float32).astype(BF16)


def f64(x):
    return np.asarray(x).astype(np.float64)


E2M1 = np.array([0.0, 0.5, 1.0, 1.5, 2.0, 3.0, 4.0, 6.0, -0.0, -0.5, -1.0, -1.5, -2.0, -3.0, -4.0, -6.0])


def pack_weight(w, fmt):
    k, n = w.shape
    w = f64(bf(w)).reshape(k // 32, 32, n)
    amax = np.abs(w).max(1)
    if fmt == "e4m3":
        byte = np.frexp(amax)[1] - 1 + 127 - 7
    else:
        mant, ex = np.frexp(amax / 6.0)
        byte = np.where(mant > 0.5, ex, ex - 1) + 127
    byte = np.clip(np.where(amax > 0, byte, 1), 1, 254)
    scaled = (w * np.exp2(127.0 - byte)[:, None, :]).reshape(k, n).astype(np.float32)
    by_word = np.ascontiguousarray(scaled.reshape(k // 512, 128, 4, n).transpose(0, 1, 3, 2))
    if fmt == "e4m3":
        words = by_word.astype(ml_dtypes.float8_e4m3fn).view(np.uint8)
    else:
        c = by_word.astype(ml_dtypes.float4_e2m1fn).view(np.uint8) & 0xF
        words = c[..., 0::2] | (c[..., 1::2] << 4)
    return np.ascontiguousarray(words), np.ascontiguousarray(byte.astype(np.uint8).reshape(k // 512, 16, n))


def unpack_weight(words, scales, fmt):
    g, p, n, _ = words.shape
    if fmt == "e4m3":
        vals = np.ascontiguousarray(words).view(ml_dtypes.float8_e4m3fn).astype(np.float64)
    else:
        nib = np.empty((g, p, n, 4), np.uint8)
        nib[..., 0::2] = words & 0xF
        nib[..., 1::2] = words >> 4
        vals = E2M1[nib]
    vals = vals * np.repeat(np.exp2(scales.astype(np.float64) - 127.0), 8, axis=1)[..., None]
    return vals.transpose(0, 1, 3, 2).reshape(g * 512, n)

def pack4(w):
    words, scales = pack_weight(w, "e2m1")
    return words.reshape(words.shape[0], 128, -1), scales


def unpack4(words, scales):
    return unpack_weight(words.reshape(words.shape[0], 128, -1, 2), scales, "e2m1")


B, C, H, W, M, O = 4, 512, 16, 16, 512, 128
N = B * H * W
L2_EPS = 1e-12
BN_EPS = 1e-5


def l2_normalize(x, axis):
    n = np.sqrt(np.sum(x * x, axis=axis, keepdims=True))
    return x / np.maximum(n, L2_EPS)


def setup_inputs():
    s = mx_kscale(C)
    cm = (np.random.standard_normal((N, C)) * 5.0 + np.random.standard_normal((1, C)) * 1.5) / np.sqrt(C)
    w = np.random.standard_normal((O, 2 * C)) * 0.1 / np.sqrt(2 * C)
    w[:, C:] = w[:, C:] / s
    words, scales = pack4(np.ascontiguousarray(w.T))
    return {"query": bf(np.random.standard_normal((B, C, H, W))), "concat_memory": bf(cm * s),
            "conv_w_words": words, "conv_w_scales": scales,
            "bn_gamma": bf(1.0 + 0.1 * np.random.standard_normal(O)), "bn_beta": bf(0.2 * np.random.standard_normal(O))}


def reference(query, concat_memory, conv_w_words, conv_w_scales, bn_gamma, bn_beta):
    q_flat = l2_normalize(f64(query), 1).transpose(0, 2, 3, 1).reshape(N, C)
    upd = np.concatenate([q_flat, f64(concat_memory)], axis=1)
    y = mxq(upd, 1, "e4m3") @ unpack4(conv_w_words, conv_w_scales)
    y = y.reshape(B, H, W, O).transpose(0, 3, 1, 2)
    mean = np.mean(y, axis=(0, 2, 3), keepdims=True)
    var = np.mean((y - mean) ** 2, axis=(0, 2, 3), keepdims=True)
    y = (y - mean) / np.sqrt(var + BN_EPS)
    y = y * f64(bn_gamma)[None, :, None, None] + f64(bn_beta)[None, :, None, None]
    return np.maximum(y, 0.0)

@@ -1,0 +1,246 @@
+from contextlib import ExitStack
+
+import concourse.mybir as mybir
+from concourse.masks import make_identity
+
+F32 = mybir.dt.float32
+BF16 = mybir.dt.bfloat16
+I32 = mybir.dt.int32
+U32 = mybir.dt.uint32
+U8 = mybir.dt.uint8
+FP8X4 = mybir.dt.float8_e4m3fn_x4
+FP4X4 = mybir.dt.float4_e2m1fn_x4
+ACT = mybir.ActivationFunctionType
+ALU = mybir.AluOpType
+
+P = 128
+PACK = 4
+BATCH = 4
+CHANNELS = 512
+PIXELS = 256
+PAIRS = PIXELS // 2
+ROWS = BATCH * PIXELS
+OUT_CH = 128
+HALF = 512
+HALVES = ROWS // HALF
+IMAGES_PER_HALF = HALF // PIXELS
+BLOCKS_PER_IMAGE = PIXELS // P
+L2_EPS = 1e-12
+BN_EPS = 1e-5
+
+FLOPS = 2 * ROWS * 2 * CHANNELS * OUT_CH
+
+
+def tile_memory_sup_pb_s_kernel(
+    tc, query, concat_memory, conv_w_words, conv_w_scales, bn_gamma, bn_beta, out
+):
+    nc = tc.nc
+    with ExitStack() as ctx:
+        keep = ctx.enter_context(tc.tile_pool(name="keep", bufs=1))
+        psum = ctx.enter_context(tc.psum_pool(name="psum", bufs=2))
+        ctx.enter_context(tc.manual_schedule())
+
+        ident_f32 = keep.tile([P, P], F32)
+        make_identity(nc, ident_f32[:])
+        minus_half = keep.tile([P, 2], F32)
+        nc.gpsimd.memset(minus_half[:], -0.5)
+        ident_bf16 = keep.tile([P, P], BF16)
+        make_identity(nc, ident_bf16[:])
+
+        one = keep.tile([P, 1], F32)
+        nc.vector.memset(one[:], 1.0)
+        gain_rows = keep.tile([P, P], BF16)
+        nc.vector.memset(gain_rows[:], 0.0)
+        w_scales = keep.tile([P, 2, OUT_CH], U8, align_bytes=64)
+        nc.vector.memset(w_scales[:].rearrange("p g n -> p (g n)").bitcast(I32), 0)
+
+        nc.scalar.dma_start(out=gain_rows[0:1, :], in_=bn_gamma.unsqueeze(0))
+        nc.scalar.dma_start(out=gain_rows[1:2, :], in_=bn_beta.unsqueeze(0))
+        warm = keep.tile([P, 1], F32)
+        nc.scalar.activation(out=warm[:], in_=one[:], func=ACT.Sqrt)
+
+        x_sb = keep.tile([P, BATCH, PACK, PIXELS], BF16)
+        mem_sb = keep.tile([P, BATCH, BLOCKS_PER_IMAGE, CHANNELS], BF16)
+        mem_view = concat_memory.rearrange("(b i r) k -> r b i k", r=P, i=BLOCKS_PER_IMAGE)
+        for b in range(BATCH):
+            nc.sync.dma_start(
+                out=x_sb[:, b], in_=query[b].rearrange("(p t) h w -> p t (h w)", t=PACK)
+            )
+            nc.sync.dma_start(out=mem_sb[:, b], in_=mem_view[:, b])
+        w_words = keep.tile([P, 2, 2 * OUT_CH], U8, align_bytes=64)
+        nc.sync.dma_start(
+            out=w_words[:].bitcast(I32), in_=conv_w_words.rearrange("g p n -> p g n").bitcast(I32)
+        )
+        for quadrant in range(4):
+            nc.sync.dma_start(
+                out=w_scales[32 * quadrant : 32 * quadrant + 4].bitcast(I32),
+                in_=conv_w_scales[:, 4 * quadrant : 4 * quadrant + 4, :]
+                .rearrange("g r n -> r g n")
+                .bitcast(I32),
+            )
+
+        sumsq = keep.tile([P, BATCH * 2], F32)
+        squares = keep.tile([P, BATCH * 2, CHANNELS], BF16)
+        clamped = keep.tile([P, BATCH * 2], F32)
+        inv_norm = keep.tile([P, BATCH * 2], F32)
+        grouped = keep.tile([P, 2, ROWS, PACK], BF16, align_bytes=64)
+        codes = keep.tile([P, 2, ROWS], U32, align_bytes=64)
+        scales = keep.tile([P, 2, ROWS], U8, align_bytes=64)
+        stats = keep.tile([P, HALVES, 6], F32)
+        y_banks = []
+        for h in range(HALVES):
+            y_bank = psum.tile([P, HALF], F32, tag="y", name="y_bank%d" % h)
+            y_banks.append(y_bank)
+        mem_banks = {}
+
+        def sum_squares(b):
+            x_t = psum.tile([P, PACK, P], F32, tag="x_t")
+            for t in range(PACK):
+                nc.tensor.transpose(x_t[:, t, :], x_sb[:, b, t, :].bitcast(F32), ident_f32[:])
+            pixel_pairs = (
+                x_t[:].rearrange("q t p -> q (t p)").bitcast(BF16).rearrange("q (c e) -> q c e", e=2)
+            )
+            for e in range(2):
+                nc.scalar.activation(
+                    out=squares[:, 2 * b + e, :],
+                    in_=pixel_pairs[:, :, e],
+                    func=ACT.Square,
+                    accum_out=sumsq[:, 2 * b + e : 2 * b + e + 1],
+                )
+
+        def invert_norm(b):
+            pair = slice(2 * b, 2 * b + 2)
+            nc.gpsimd.tensor_scalar_max(out=clamped[:, pair], in0=sumsq[:, pair], scalar1=L2_EPS * L2_EPS)
+            nc.gpsimd.tensor_tensor(out=inv_norm[:, pair], in0=clamped[:, pair], in1=minus_half[:], op=ALU.pow)
+
+        def normalise(b):
+            spread = psum.tile([P, HALF], F32, tag="spread")
+            for e in range(2):
+                nc.tensor.transpose(
+                    spread[:, e * PAIRS : (e + 1) * PAIRS],
+                    inv_norm[:, 2 * b + e : 2 * b + e + 1].to_broadcast([P, P]),
+                    ident_f32[:],
+                )
+            nc.vector.tensor_tensor(
+                out=grouped[:, 0, b * PIXELS : (b + 1) * PIXELS, :].rearrange("p (q e) t -> p q e t", e=2),
+                in0=x_sb[:, b].rearrange("p t (q e) -> p q e t", e=2),
+                in1=spread[:, 0:PIXELS]
+                .rearrange("p (e q) -> p q e", e=2)
+                .unsqueeze(3)
+                .to_broadcast([P, PAIRS, 2, PACK]),
+                op=ALU.mult,
+            )
+
+        def transpose_memory(b):
+            m_t = psum.tile([P, BLOCKS_PER_IMAGE, 2, P], F32, tag="m_t", name="m_t%d" % b)
+            for i in range(BLOCKS_PER_IMAGE):
+                words = mem_sb[:, b, i, :].bitcast(F32)
+                for u in range(2):
+                    nc.tensor.transpose(m_t[:, i, u, :], words[:, u : CHANNELS // 2 : 2], ident_f32[:])
+            mem_banks[b] = m_t
+
+        def group_memory(copy, b):
+            copy(
+                out=grouped[:, 1, b * PIXELS : (b + 1) * PIXELS, :]
+                .bitcast(F32)
+                .rearrange("p (i r) u -> p i r u", i=BLOCKS_PER_IMAGE),
+                in_=mem_banks[b][:].rearrange("p i u r -> p i r u"),
+            )
+
+        def quantise(g, b):
+            cols = slice(b * PIXELS, (b + 1) * PIXELS)
+            nc.vector.quantize_mx(
+                out=codes[:, g, cols].bitcast(FP8X4),
+                scales=scales[:, g, cols],
+                in_=grouped[:, g, cols, :].rearrange("p n t -> p (n t)"),
+            )
+
+        def multiply(g, h, start, stop):
+            cols = slice(h * HALF, (h + 1) * HALF)
+            nc.tensor.matmul_mx(
+                out=y_banks[h][:],
+                lhsT=w_words[:, g, :].bitcast(FP4X4),
+                lhsT_scale=w_scales[:, g, :],
+                rhs=codes[:, g, cols].bitcast(FP8X4),
+                rhs_scale=scales[:, g, cols],
+                start=start,
+                stop=stop,
+            )
+
+        first_half = range(IMAGES_PER_HALF)
+        second_half = range(IMAGES_PER_HALF, BATCH)
+
+        for b in first_half:
+            sum_squares(b)
+            transpose_memory(b)
+            invert_norm(b)
+            group_memory(nc.vector.tensor_copy, b)
+        gain_t = psum.tile([P, 2 * HALF], BF16, tag="spread")
+        nc.tensor.transpose(gain_t[:, 0:P], gain_rows[:], ident_bf16[:])
+        gamma_pm = keep.tile([P, 2], F32)
+        nc.vector.tensor_copy(out=gamma_pm[:, 0:1], in_=gain_t[:, 0:1])
+        nc.vector.tensor_scalar_mul(out=gamma_pm[:, 1:2], in0=gain_t[:, 0:1], scalar1=-1.0)
+        beta = keep.tile([P, 1], F32)
+        nc.vector.tensor_copy(out=beta[:], in_=gain_t[:, 1:2])
+        for b in first_half:
+            quantise(1, b)
+
+        for b in second_half:
+            sum_squares(b)
+            transpose_memory(b)
+            invert_norm(b)
+            normalise(b - IMAGES_PER_HALF)
+        for b in first_half:
+            quantise(0, b)
+        for b in second_half:
+            group_memory(nc.scalar.copy, b)
+
+        for b in second_half:
+            normalise(b)
+            if b == IMAGES_PER_HALF:
+                multiply(1, 0, True, False)
+                multiply(0, 0, False, True)
+        for b in second_half:
+            quantise(1, b)
+            quantise(0, b)
+        multiply(1, 1, True, False)
+        multiply(0, 1, False, True)
+        for h in range(HALVES):
+            nc.vector.bn_stats(out=stats[:, h, :], in_=y_banks[h][:])
+
+        mean_var = keep.tile([P, 2], F32)
+        nc.vector.bn_aggr(out=mean_var[:], in_=stats[:].rearrange("p h s -> p (h s)"))
+        std = keep.tile([P, 1], F32)
+        nc.scalar.activation(out=std[:], in_=mean_var[:, 1:2], func=ACT.Sqrt, bias=BN_EPS)
+        inv_std = keep.tile([P, 1], F32)
+        nc.vector.reciprocal(out=inv_std[:], in_=std[:])
+        scale_pm = keep.tile([P, 2], F32)
+        nc.vector.tensor_scalar_mul(out=scale_pm[:], in0=gamma_pm[:], scalar1=inv_std[:])
+        shift = keep.tile([P, 1], F32)
+        nc.vector.tensor_scalar(
+            out=shift[:],
+            in0=mean_var[:, 0:1],
+            scalar1=scale_pm[:, 1:2],
+            scalar2=beta[:],
+            op0=ALU.mult,
+            op1=ALU.add,
+        )
+        out_view = out.rearrange("b o h w -> o b (h w)")
+        result = keep.tile([P, HALVES, HALF], F32)
+        nc.scalar.activation(
+            out=result[:, 0, :], in_=y_banks[0][:], func=ACT.Relu, bias=shift[:], scale=scale_pm[:, 0:1]
+        )
+        nc.vector.tensor_scalar(
+            out=result[:, 1, :],
+            in0=y_banks[1][:],
+            scalar1=scale_pm[:, 0:1],
+            scalar2=shift[:],
+            op0=ALU.mult,
+            op1=ALU.add,
+        )
+        nc.vector.tensor_scalar_max(out=result[:, 1, :], in0=result[:, 1, :], scalar1=0.0)
+        for h in range(HALVES):
+            nc.sync.dma_start(
+                out=out_view[:, h * IMAGES_PER_HALF : (h + 1) * IMAGES_PER_HALF, :],
+                in_=result[:, h, :].rearrange("o (b n) -> o b n", b=IMAGES_PER_HALF),
+            )

@@ -24,7 +24,6 @@ OUT_CH = 128
 HALF = 512
 HALVES = ROWS // HALF
 IMAGES_PER_HALF = HALF // PIXELS
-BLOCKS_PER_IMAGE = PIXELS // P
 L2_EPS = 1e-12
 BN_EPS = 1e-5
 
@@ -57,16 +56,29 @@ def tile_memory_sup_pb_s_kernel(
         nc.scalar.dma_start(out=gain_rows[0:1, :], in_=bn_gamma.unsqueeze(0))
         nc.scalar.dma_start(out=gain_rows[1:2, :], in_=bn_beta.unsqueeze(0))
         warm = keep.tile([P, 1], F32)
-        nc.scalar.activation(out=warm[:], in_=one[:], func=ACT.Sqrt)
+        nc.scalar.activation(out=warm[:], in_=one[:], func=ACT.Abs_reciprocal_sqrt)
 
+        first_half = range(IMAGES_PER_HALF)
+        second_half = range(IMAGES_PER_HALF, BATCH)
         x_sb = keep.tile([P, BATCH, PACK, PIXELS], BF16)
-        mem_sb = keep.tile([P, BATCH, BLOCKS_PER_IMAGE, CHANNELS], BF16)
-        mem_view = concat_memory.rearrange("(b i r) k -> r b i k", r=P, i=BLOCKS_PER_IMAGE)
-        for b in range(BATCH):
+        mem_sb = keep.tile([P, BATCH, 2, CHANNELS], BF16)
+        mem_view = concat_memory.rearrange("(b q e) k -> q b e k", q=PAIRS, e=2)
+
+        def load_image(b):
             nc.sync.dma_start(
                 out=x_sb[:, b], in_=query[b].rearrange("(p t) h w -> p t (h w)", t=PACK)
             )
+
+        def load_memory(b):
             nc.sync.dma_start(out=mem_sb[:, b], in_=mem_view[:, b])
+
+        for b in first_half:
+            load_image(b)
+            load_memory(b)
+        for b in second_half:
+            load_image(b)
+        for b in second_half:
+            load_memory(b)
         w_words = keep.tile([P, 2, 2 * OUT_CH], U8, align_bytes=64)
         nc.sync.dma_start(
             out=w_words[:].bitcast(I32), in_=conv_w_words.rearrange("g p n -> p g n").bitcast(I32)
@@ -132,19 +144,19 @@ def tile_memory_sup_pb_s_kernel(
             )
 
         def transpose_memory(b):
-            m_t = psum.tile([P, BLOCKS_PER_IMAGE, 2, P], F32, tag="m_t", name="m_t%d" % b)
-            for i in range(BLOCKS_PER_IMAGE):
-                words = mem_sb[:, b, i, :].bitcast(F32)
+            m_t = psum.tile([P, 2, 2, PAIRS], F32, tag="m_t", name="m_t%d" % b)
+            for e in range(2):
+                words = mem_sb[:, b, e, :].bitcast(F32)
                 for u in range(2):
-                    nc.tensor.transpose(m_t[:, i, u, :], words[:, u : CHANNELS // 2 : 2], ident_f32[:])
+                    nc.tensor.transpose(m_t[:, e, u, :], words[:, u : CHANNELS // 2 : 2], ident_f32[:])
             mem_banks[b] = m_t
 
         def group_memory(copy, b):
             copy(
                 out=grouped[:, 1, b * PIXELS : (b + 1) * PIXELS, :]
                 .bitcast(F32)
-                .rearrange("p (i r) u -> p i r u", i=BLOCKS_PER_IMAGE),
-                in_=mem_banks[b][:].rearrange("p i u r -> p i r u"),
+                .rearrange("p (q e) u -> p q e u", e=2),
+                in_=mem_banks[b][:].rearrange("p e u q -> p q e u"),
             )
 
         def quantise(g, b):
@@ -167,9 +179,6 @@ def tile_memory_sup_pb_s_kernel(
                 stop=stop,
             )
 
-        first_half = range(IMAGES_PER_HALF)
-        second_half = range(IMAGES_PER_HALF, BATCH)
-
         for b in first_half:
             sum_squares(b)
             transpose_memory(b)
@@ -187,33 +196,28 @@ def tile_memory_sup_pb_s_kernel(
 
         for b in second_half:
             sum_squares(b)
-            transpose_memory(b)
             invert_norm(b)
             normalise(b - IMAGES_PER_HALF)
         for b in first_half:
             quantise(0, b)
-        for b in second_half:
-            group_memory(nc.scalar.copy, b)
 
         for b in second_half:
             normalise(b)
-            if b == IMAGES_PER_HALF:
-                multiply(1, 0, True, False)
-                multiply(0, 0, False, True)
+            transpose_memory(b)
+            group_memory(nc.scalar.copy, b)
         for b in second_half:
             quantise(1, b)
             quantise(0, b)
-        multiply(1, 1, True, False)
-        multiply(0, 1, False, True)
+
         for h in range(HALVES):
+            multiply(1, h, True, False)
+            multiply(0, h, False, True)
             nc.vector.bn_stats(out=stats[:, h, :], in_=y_banks[h][:])
 
         mean_var = keep.tile([P, 2], F32)
         nc.vector.bn_aggr(out=mean_var[:], in_=stats[:].rearrange("p h s -> p (h s)"))
-        std = keep.tile([P, 1], F32)
-        nc.scalar.activation(out=std[:], in_=mean_var[:, 1:2], func=ACT.Sqrt, bias=BN_EPS)
         inv_std = keep.tile([P, 1], F32)
-        nc.vector.reciprocal(out=inv_std[:], in_=std[:])
+        nc.scalar.activation(out=inv_std[:], in_=mean_var[:, 1:2], func=ACT.Abs_reciprocal_sqrt, bias=BN_EPS)
         scale_pm = keep.tile([P, 2], F32)
         nc.vector.tensor_scalar_mul(out=scale_pm[:], in0=gamma_pm[:], scalar1=inv_std[:])
         shift = keep.tile([P, 1], F32)

@@ -53,8 +53,6 @@ def tile_memory_sup_pb_s_kernel(
         w_scales = keep.tile([P, 2, OUT_CH], U8, align_bytes=64)
         nc.vector.memset(w_scales[:].rearrange("p g n -> p (g n)").bitcast(I32), 0)
 
-        nc.scalar.dma_start(out=gain_rows[0:1, :], in_=bn_gamma.unsqueeze(0))
-        nc.scalar.dma_start(out=gain_rows[1:2, :], in_=bn_beta.unsqueeze(0))
         warm = keep.tile([P, 1], F32)
         nc.scalar.activation(out=warm[:], in_=one[:], func=ACT.Abs_reciprocal_sqrt)
 
@@ -64,19 +62,20 @@ def tile_memory_sup_pb_s_kernel(
         mem_sb = keep.tile([P, BATCH, 2, CHANNELS], BF16)
         mem_view = concat_memory.rearrange("(b q e) k -> q b e k", q=PAIRS, e=2)
 
-        def load_image(b):
-            nc.sync.dma_start(
-                out=x_sb[:, b], in_=query[b].rearrange("(p t) h w -> p t (h w)", t=PACK)
-            )
+        def load_image(b, pieces):
+            channels = query[b].rearrange("(p t) h w -> p t (h w)", t=PACK)
+            step = PACK // pieces
+            for t in range(0, PACK, step):
+                nc.sync.dma_start(out=x_sb[:, b, t : t + step], in_=channels[:, t : t + step])
 
         def load_memory(b):
             nc.sync.dma_start(out=mem_sb[:, b], in_=mem_view[:, b])
 
         for b in first_half:
-            load_image(b)
+            load_image(b, pieces=2 if b == 0 else 1)
             load_memory(b)
         for b in second_half:
-            load_image(b)
+            load_image(b, pieces=1)
         for b in second_half:
             load_memory(b)
         w_words = keep.tile([P, 2, 2 * OUT_CH], U8, align_bytes=64)
@@ -90,6 +89,8 @@ def tile_memory_sup_pb_s_kernel(
                 .rearrange("g r n -> r g n")
                 .bitcast(I32),
             )
+        nc.sync.dma_start(out=gain_rows[0:1, :], in_=bn_gamma.unsqueeze(0))
+        nc.sync.dma_start(out=gain_rows[1:2, :], in_=bn_beta.unsqueeze(0))
 
         sumsq = keep.tile([P, BATCH * 2], F32)
         squares = keep.tile([P, BATCH * 2, CHANNELS], BF16)
@@ -184,13 +185,6 @@ def tile_memory_sup_pb_s_kernel(
             transpose_memory(b)
             invert_norm(b)
             group_memory(nc.vector.tensor_copy, b)
-        gain_t = psum.tile([P, 2 * HALF], BF16, tag="spread")
-        nc.tensor.transpose(gain_t[:, 0:P], gain_rows[:], ident_bf16[:])
-        gamma_pm = keep.tile([P, 2], F32)
-        nc.vector.tensor_copy(out=gamma_pm[:, 0:1], in_=gain_t[:, 0:1])
-        nc.vector.tensor_scalar_mul(out=gamma_pm[:, 1:2], in0=gain_t[:, 0:1], scalar1=-1.0)
-        beta = keep.tile([P, 1], F32)
-        nc.vector.tensor_copy(out=beta[:], in_=gain_t[:, 1:2])
         for b in first_half:
             quantise(1, b)
 
@@ -207,7 +201,16 @@ def tile_memory_sup_pb_s_kernel(
             group_memory(nc.scalar.copy, b)
         for b in second_half:
             quantise(1, b)
+        for b in second_half:
             quantise(0, b)
+
+        gain_t = psum.tile([P, 2 * HALF], BF16, tag="spread")
+        nc.tensor.transpose(gain_t[:, 0:P], gain_rows[:], ident_bf16[:])
+        gamma_pm = keep.tile([P, 2], F32)
+        nc.vector.tensor_copy(out=gamma_pm[:, 0:1], in_=gain_t[:, 0:1])
+        nc.vector.tensor_scalar_mul(out=gamma_pm[:, 1:2], in0=gain_t[:, 0:1], scalar1=-1.0)
+        beta = keep.tile([P, 1], F32)
+        nc.vector.tensor_copy(out=beta[:], in_=gain_t[:, 1:2])
 
         for h in range(HALVES):
             multiply(1, h, True, False)

@@ -24,6 +24,7 @@ OUT_CH = 128
 HALF = 512
 HALVES = ROWS // HALF
 IMAGES_PER_HALF = HALF // PIXELS
+PLANES = BATCH * 2
 L2_EPS = 1e-12
 BN_EPS = 1e-5
 
@@ -41,7 +42,7 @@ def tile_memory_sup_pb_s_kernel(
 
         ident_f32 = keep.tile([P, P], F32)
         make_identity(nc, ident_f32[:])
-        minus_half = keep.tile([P, 2], F32)
+        minus_half = keep.tile([P, 1], F32)
         nc.gpsimd.memset(minus_half[:], -0.5)
         ident_bf16 = keep.tile([P, P], BF16)
         make_identity(nc, ident_bf16[:])
@@ -56,8 +57,6 @@ def tile_memory_sup_pb_s_kernel(
         warm = keep.tile([P, 1], F32)
         nc.scalar.activation(out=warm[:], in_=one[:], func=ACT.Abs_reciprocal_sqrt)
 
-        first_half = range(IMAGES_PER_HALF)
-        second_half = range(IMAGES_PER_HALF, BATCH)
         x_sb = keep.tile([P, BATCH, PACK, PIXELS], BF16)
         mem_sb = keep.tile([P, BATCH, 2, CHANNELS], BF16)
         mem_view = concat_memory.rearrange("(b q e) k -> q b e k", q=PAIRS, e=2)
@@ -71,12 +70,8 @@ def tile_memory_sup_pb_s_kernel(
         def load_memory(b):
             nc.sync.dma_start(out=mem_sb[:, b], in_=mem_view[:, b])
 
-        for b in first_half:
+        for b in range(BATCH):
             load_image(b, pieces=2 if b == 0 else 1)
-            load_memory(b)
-        for b in second_half:
-            load_image(b, pieces=1)
-        for b in second_half:
             load_memory(b)
         w_words = keep.tile([P, 2, 2 * OUT_CH], U8, align_bytes=64)
         nc.sync.dma_start(
@@ -92,22 +87,18 @@ def tile_memory_sup_pb_s_kernel(
         nc.sync.dma_start(out=gain_rows[0:1, :], in_=bn_gamma.unsqueeze(0))
         nc.sync.dma_start(out=gain_rows[1:2, :], in_=bn_beta.unsqueeze(0))
 
-        sumsq = keep.tile([P, BATCH * 2], F32)
-        squares = keep.tile([P, BATCH * 2, CHANNELS], BF16)
-        clamped = keep.tile([P, BATCH * 2], F32)
-        inv_norm = keep.tile([P, BATCH * 2], F32)
+        sumsq = keep.tile([P, PLANES], F32)
+        squares = keep.tile([P, PLANES, CHANNELS], BF16)
+        inv_norm = keep.tile([P, PLANES], F32)
         grouped = keep.tile([P, 2, ROWS, PACK], BF16, align_bytes=64)
         codes = keep.tile([P, 2, ROWS], U32, align_bytes=64)
         scales = keep.tile([P, 2, ROWS], U8, align_bytes=64)
         stats = keep.tile([P, HALVES, 6], F32)
         y_banks = []
-        for h in range(HALVES):
-            y_bank = psum.tile([P, HALF], F32, tag="y", name="y_bank%d" % h)
-            y_banks.append(y_bank)
         mem_banks = {}
 
         def sum_squares(b):
-            x_t = psum.tile([P, PACK, P], F32, tag="x_t")
+            x_t = psum.tile([P, PACK, P], F32, tag="x_t_then_y")
             for t in range(PACK):
                 nc.tensor.transpose(x_t[:, t, :], x_sb[:, b, t, :].bitcast(F32), ident_f32[:])
             pixel_pairs = (
@@ -121,31 +112,27 @@ def tile_memory_sup_pb_s_kernel(
                     accum_out=sumsq[:, 2 * b + e : 2 * b + e + 1],
                 )
 
-        def invert_norm(b):
-            pair = slice(2 * b, 2 * b + 2)
-            nc.gpsimd.tensor_scalar_max(out=clamped[:, pair], in0=sumsq[:, pair], scalar1=L2_EPS * L2_EPS)
-            nc.gpsimd.tensor_tensor(out=inv_norm[:, pair], in0=clamped[:, pair], in1=minus_half[:], op=ALU.pow)
-
-        def normalise(b):
+        def normalise(b, e):
+            plane = 2 * b + e
+            column = slice(plane, plane + 1)
+            nc.gpsimd.tensor_tensor(
+                out=inv_norm[:, column], in0=sumsq[:, column], in1=minus_half[:], op=ALU.pow
+            )
             spread = psum.tile([P, HALF], F32, tag="spread")
-            for e in range(2):
-                nc.tensor.transpose(
-                    spread[:, e * PAIRS : (e + 1) * PAIRS],
-                    inv_norm[:, 2 * b + e : 2 * b + e + 1].to_broadcast([P, P]),
-                    ident_f32[:],
-                )
-            nc.vector.tensor_tensor(
-                out=grouped[:, 0, b * PIXELS : (b + 1) * PIXELS, :].rearrange("p (q e) t -> p q e t", e=2),
-                in0=x_sb[:, b].rearrange("p t (q e) -> p q e t", e=2),
-                in1=spread[:, 0:PIXELS]
-                .rearrange("p (e q) -> p q e", e=2)
-                .unsqueeze(3)
-                .to_broadcast([P, PAIRS, 2, PACK]),
-                op=ALU.mult,
+            nc.tensor.transpose(
+                spread[:, 0:PAIRS], inv_norm[:, column].to_broadcast([P, P]), ident_f32[:]
+            )
+            nc.vector.scalar_tensor_tensor(
+                out=grouped[:, 0, plane * PAIRS : (plane + 1) * PAIRS, :],
+                in0=spread[:, 0:PAIRS].unsqueeze(2).to_broadcast([P, PAIRS, PACK]),
+                scalar=1.0 / L2_EPS,
+                in1=x_sb[:, b].rearrange("p t (q e) -> p e q t", e=2)[:, e],
+                op0=ALU.min,
+                op1=ALU.mult,
             )
 
         def transpose_memory(b):
-            m_t = psum.tile([P, 2, 2, PAIRS], F32, tag="m_t", name="m_t%d" % b)
+            m_t = psum.tile([P, 2, 2, PAIRS], F32, tag="m_t", name="m_t%d" % b, bufs=BATCH)
             for e in range(2):
                 words = mem_sb[:, b, e, :].bitcast(F32)
                 for u in range(2):
@@ -156,8 +143,8 @@ def tile_memory_sup_pb_s_kernel(
             copy(
                 out=grouped[:, 1, b * PIXELS : (b + 1) * PIXELS, :]
                 .bitcast(F32)
-                .rearrange("p (q e) u -> p q e u", e=2),
-                in_=mem_banks[b][:].rearrange("p e u q -> p q e u"),
+                .rearrange("p (e q) u -> p e q u", e=2),
+                in_=mem_banks[b][:].rearrange("p e u q -> p e q u"),
             )
 
         def quantise(g, b):
@@ -180,72 +167,81 @@ def tile_memory_sup_pb_s_kernel(
                 stop=stop,
             )
 
-        for b in first_half:
-            sum_squares(b)
-            transpose_memory(b)
-            invert_norm(b)
-            group_memory(nc.vector.tensor_copy, b)
-        for b in first_half:
-            quantise(1, b)
-
-        for b in second_half:
-            sum_squares(b)
-            invert_norm(b)
-            normalise(b - IMAGES_PER_HALF)
-        for b in first_half:
-            quantise(0, b)
-
-        for b in second_half:
-            normalise(b)
-            transpose_memory(b)
+        sum_squares(0)
+        transpose_memory(0)
+        group_memory(nc.vector.tensor_copy, 0)
+        quantise(1, 0)
+        sum_squares(1)
+        for b in range(BATCH):
+            normalise(b, 0)
+            if b > 0:
+                quantise(0, b - 1)
+            if b + 1 < BATCH:
+                transpose_memory(b + 1)
+            normalise(b, 1)
+            if b + 2 < BATCH:
+                sum_squares(b + 2)
+        for b in range(1, BATCH):
             group_memory(nc.scalar.copy, b)
-        for b in second_half:
+        quantise(1, 1)
+        quantise(0, BATCH - 1)
+        for b in range(IMAGES_PER_HALF, BATCH):
             quantise(1, b)
-        for b in second_half:
-            quantise(0, b)
 
         gain_t = psum.tile([P, 2 * HALF], BF16, tag="spread")
         nc.tensor.transpose(gain_t[:, 0:P], gain_rows[:], ident_bf16[:])
-        gamma_pm = keep.tile([P, 2], F32)
-        nc.vector.tensor_copy(out=gamma_pm[:, 0:1], in_=gain_t[:, 0:1])
-        nc.vector.tensor_scalar_mul(out=gamma_pm[:, 1:2], in0=gain_t[:, 0:1], scalar1=-1.0)
-        beta = keep.tile([P, 1], F32)
-        nc.vector.tensor_copy(out=beta[:], in_=gain_t[:, 1:2])
+        gamma_and_u = keep.tile([P, 2], F32)
+        nc.vector.tensor_copy(out=gamma_and_u[:, 0:1], in_=gain_t[:, 0:1])
+        minus_gamma = keep.tile([P, 1], F32)
+        nc.vector.tensor_scalar_mul(out=minus_gamma[:], in0=gain_t[:, 0:1], scalar1=-1.0)
+        zero_and_beta = keep.tile([P, 2], F32)
+        nc.vector.memset(zero_and_beta[:, 0:1], 0.0)
+        nc.vector.tensor_copy(out=zero_and_beta[:, 1:2], in_=gain_t[:, 1:2])
 
         for h in range(HALVES):
-            multiply(1, h, True, False)
-            multiply(0, h, False, True)
+            y_bank = psum.tile([P, HALF], F32, tag="x_t_then_y", name="y_bank%d" % h)
+            y_banks.append(y_bank)
+            multiply(0, h, True, False)
+            multiply(1, h, False, True)
             nc.vector.bn_stats(out=stats[:, h, :], in_=y_banks[h][:])
 
         mean_var = keep.tile([P, 2], F32)
         nc.vector.bn_aggr(out=mean_var[:], in_=stats[:].rearrange("p h s -> p (h s)"))
         inv_std = keep.tile([P, 1], F32)
         nc.scalar.activation(out=inv_std[:], in_=mean_var[:, 1:2], func=ACT.Abs_reciprocal_sqrt, bias=BN_EPS)
-        scale_pm = keep.tile([P, 2], F32)
-        nc.vector.tensor_scalar_mul(out=scale_pm[:], in0=gamma_pm[:], scalar1=inv_std[:])
-        shift = keep.tile([P, 1], F32)
-        nc.vector.tensor_scalar(
-            out=shift[:],
-            in0=mean_var[:, 0:1],
-            scalar1=scale_pm[:, 1:2],
-            scalar2=beta[:],
+        nc.vector.tensor_scalar_mul(out=gamma_and_u[:, 1:2], in0=mean_var[:, 0:1], scalar1=minus_gamma[:])
+        scale_shift = keep.tile([P, 2], F32)
+        nc.vector.scalar_tensor_tensor(
+            out=scale_shift[:],
+            in0=gamma_and_u[:],
+            scalar=inv_std[:],
+            in1=zero_and_beta[:],
             op0=ALU.mult,
             op1=ALU.add,
         )
-        out_view = out.rearrange("b o h w -> o b (h w)")
+        scale = scale_shift[:, 0:1]
+        shift = scale_shift[:, 1:2]
         result = keep.tile([P, HALVES, HALF], F32)
+
+        def in_pixel_order(bank):
+            return bank.rearrange("o (b e q) -> o b q e", b=IMAGES_PER_HALF, e=2)
+
+        def as_written(bank):
+            return bank.rearrange("o (b q e) -> o b q e", b=IMAGES_PER_HALF, e=2)
+
         nc.scalar.activation(
-            out=result[:, 0, :], in_=y_banks[0][:], func=ACT.Relu, bias=shift[:], scale=scale_pm[:, 0:1]
+            out=as_written(result[:, 0, :]), in_=in_pixel_order(y_banks[0][:]), func=ACT.Relu, bias=shift, scale=scale
         )
         nc.vector.tensor_scalar(
-            out=result[:, 1, :],
-            in0=y_banks[1][:],
-            scalar1=scale_pm[:, 0:1],
-            scalar2=shift[:],
+            out=as_written(result[:, 1, :]),
+            in0=in_pixel_order(y_banks[1][:]),
+            scalar1=scale,
+            scalar2=shift,
             op0=ALU.mult,
             op1=ALU.add,
         )
         nc.vector.tensor_scalar_max(out=result[:, 1, :], in0=result[:, 1, :], scalar1=0.0)
+        out_view = out.rearrange("b o h w -> o b (h w)")
         for h in range(HALVES):
             nc.sync.dma_start(
                 out=out_view[:, h * IMAGES_PER_HALF : (h + 1) * IMAGES_PER_HALF, :],

@@ -22,9 +22,8 @@ PAIRS = PIXELS // 2
 ROWS = BATCH * PIXELS
 OUT_CH = 128
 HALF = 512
-HALVES = ROWS // HALF
-IMAGES_PER_HALF = HALF // PIXELS
 PLANES = BATCH * 2
+SCALAR_STATS = 2
 L2_EPS = 1e-12
 BN_EPS = 1e-5
 
@@ -42,8 +41,6 @@ def tile_memory_sup_pb_s_kernel(
 
         ident_f32 = keep.tile([P, P], F32)
         make_identity(nc, ident_f32[:])
-        minus_half = keep.tile([P, 1], F32)
-        nc.gpsimd.memset(minus_half[:], -0.5)
         ident_bf16 = keep.tile([P, P], BF16)
         make_identity(nc, ident_bf16[:])
 
@@ -93,38 +90,52 @@ def tile_memory_sup_pb_s_kernel(
         grouped = keep.tile([P, 2, ROWS, PACK], BF16, align_bytes=64)
         codes = keep.tile([P, 2, ROWS], U32, align_bytes=64)
         scales = keep.tile([P, 2, ROWS], U8, align_bytes=64)
-        stats = keep.tile([P, HALVES, 6], F32)
+        stats = keep.tile([P, SCALAR_STATS * 3 + (BATCH - SCALAR_STATS) * 6], F32)
+        nc.vector.memset(stats[:, 0 : 3 * SCALAR_STATS], float(PIXELS))
+        unread = keep.tile([P, SCALAR_STATS, 2, PIXELS], F32)
+        gamma_and_u = keep.tile([P, 2], F32)
+        minus_gamma = keep.tile([P, 1], F32)
+        zero_and_beta = keep.tile([P, 2], F32)
+        nc.vector.memset(zero_and_beta[:, 0:1], 0.0)
         y_banks = []
         mem_banks = {}
+        query_banks = []
+        spread_banks = {}
 
-        def sum_squares(b):
-            x_t = psum.tile([P, PACK, P], F32, tag="x_t_then_y")
+        def transpose_query(b):
+            x_t = psum.tile([P, PACK, P], F32, tag="x_t")
             for t in range(PACK):
                 nc.tensor.transpose(x_t[:, t, :], x_sb[:, b, t, :].bitcast(F32), ident_f32[:])
-            pixel_pairs = (
-                x_t[:].rearrange("q t p -> q (t p)").bitcast(BF16).rearrange("q (c e) -> q c e", e=2)
-            )
-            for e in range(2):
-                nc.scalar.activation(
-                    out=squares[:, 2 * b + e, :],
-                    in_=pixel_pairs[:, :, e],
-                    func=ACT.Square,
-                    accum_out=sumsq[:, 2 * b + e : 2 * b + e + 1],
-                )
+            query_banks.append(x_t)
 
-        def normalise(b, e):
-            plane = 2 * b + e
-            column = slice(plane, plane + 1)
-            nc.gpsimd.tensor_tensor(
-                out=inv_norm[:, column], in0=sumsq[:, column], in1=minus_half[:], op=ALU.pow
+        def sum_squares(plane):
+            b, e = divmod(plane, 2)
+            pixel_pairs = (
+                query_banks[b][:].rearrange("q t p -> q (t p)").bitcast(BF16).rearrange("q (c e) -> q c e", e=2)
             )
+            nc.scalar.activation(
+                out=squares[:, plane, :],
+                in_=pixel_pairs[:, :, e],
+                func=ACT.Square,
+                accum_out=sumsq[:, plane : plane + 1],
+            )
+
+        def invert_norm(plane):
+            column = slice(plane, plane + 1)
+            nc.scalar.activation(out=inv_norm[:, column], in_=sumsq[:, column], func=ACT.Abs_reciprocal_sqrt)
+
+        def spread_norm(plane):
             spread = psum.tile([P, HALF], F32, tag="spread")
             nc.tensor.transpose(
-                spread[:, 0:PAIRS], inv_norm[:, column].to_broadcast([P, P]), ident_f32[:]
+                spread[:, 0:PAIRS], inv_norm[:, plane : plane + 1].to_broadcast([P, P]), ident_f32[:]
             )
+            spread_banks[plane] = spread
+
+        def normalise(plane):
+            b, e = divmod(plane, 2)
             nc.vector.scalar_tensor_tensor(
                 out=grouped[:, 0, plane * PAIRS : (plane + 1) * PAIRS, :],
-                in0=spread[:, 0:PAIRS].unsqueeze(2).to_broadcast([P, PAIRS, PACK]),
+                in0=spread_banks[plane][:, 0:PAIRS].unsqueeze(2).to_broadcast([P, PAIRS, PACK]),
                 scalar=1.0 / L2_EPS,
                 in1=x_sb[:, b].rearrange("p t (q e) -> p e q t", e=2)[:, e],
                 op0=ALU.min,
@@ -132,7 +143,7 @@ def tile_memory_sup_pb_s_kernel(
             )
 
         def transpose_memory(b):
-            m_t = psum.tile([P, 2, 2, PAIRS], F32, tag="m_t", name="m_t%d" % b, bufs=BATCH)
+            m_t = psum.tile([P, 2, 2, PAIRS], F32, tag="m_t_then_y", name="m_t%d" % b, bufs=BATCH)
             for e in range(2):
                 words = mem_sb[:, b, e, :].bitcast(F32)
                 for u in range(2):
@@ -155,58 +166,108 @@ def tile_memory_sup_pb_s_kernel(
                 in_=grouped[:, g, cols, :].rearrange("p n t -> p (n t)"),
             )
 
-        def multiply(g, h, start, stop):
-            cols = slice(h * HALF, (h + 1) * HALF)
-            nc.tensor.matmul_mx(
-                out=y_banks[h][:],
-                lhsT=w_words[:, g, :].bitcast(FP4X4),
-                lhsT_scale=w_scales[:, g, :],
-                rhs=codes[:, g, cols].bitcast(FP8X4),
-                rhs_scale=scales[:, g, cols],
-                start=start,
-                stop=stop,
-            )
+        def multiply(b):
+            y_bank = psum.tile([P, PIXELS], F32, tag="m_t_then_y", name="y_bank%d" % b, bufs=BATCH)
+            y_banks.append(y_bank)
+            for e in range(2):
+                cols = slice((2 * b + e) * PAIRS, (2 * b + e + 1) * PAIRS)
+                for g in (1, 0):
+                    nc.tensor.matmul_mx(
+                        out=y_bank[:, e * PAIRS : (e + 1) * PAIRS],
+                        lhsT=w_words[:, g, :].bitcast(FP4X4),
+                        lhsT_scale=w_scales[:, g, :],
+                        rhs=codes[:, g, cols].bitcast(FP8X4),
+                        rhs_scale=scales[:, g, cols],
+                        start=(g == 1),
+                        stop=(g == 0),
+                    )
 
+        def statistics(b):
+            if b < SCALAR_STATS:
+                mean = stats[:, 3 * b + 1 : 3 * b + 2]
+                nc.scalar.activation(
+                    out=unread[:, b, 0, :], in_=y_banks[b][:], func=ACT.Identity, scale=1.0 / PIXELS, accum_out=mean
+                )
+                nc.scalar.activation(
+                    out=unread[:, b, 1, :],
+                    in_=y_banks[b][:],
+                    func=ACT.Square,
+                    scale=-1.0,
+                    bias=mean,
+                    accum_out=stats[:, 3 * b + 2 : 3 * b + 3],
+                )
+            else:
+                first = 3 * SCALAR_STATS + 6 * (b - SCALAR_STATS)
+                nc.vector.bn_stats(out=stats[:, first : first + 6], in_=y_banks[b][:])
+
+        transpose_query(0)
         sum_squares(0)
+        invert_norm(0)
         transpose_memory(0)
         group_memory(nc.vector.tensor_copy, 0)
         quantise(1, 0)
+        transpose_query(1)
+        spread_norm(0)
+        normalise(0)
         sum_squares(1)
-        for b in range(BATCH):
-            normalise(b, 0)
-            if b > 0:
-                quantise(0, b - 1)
-            if b + 1 < BATCH:
-                transpose_memory(b + 1)
-            normalise(b, 1)
-            if b + 2 < BATCH:
-                sum_squares(b + 2)
-        for b in range(1, BATCH):
-            group_memory(nc.scalar.copy, b)
+        invert_norm(1)
+        transpose_memory(1)
+        spread_norm(1)
+        normalise(1)
+        group_memory(nc.vector.tensor_copy, 1)
+        transpose_query(2)
+        sum_squares(2)
+        sum_squares(3)
+        invert_norm(2)
+        spread_norm(2)
+        normalise(2)
+        quantise(0, 0)
+        transpose_query(3)
+        sum_squares(4)
+        invert_norm(3)
+        spread_norm(3)
+        normalise(3)
+        transpose_memory(2)
+        sum_squares(5)
+        invert_norm(4)
+        spread_norm(4)
+        normalise(4)
+        quantise(0, 1)
         quantise(1, 1)
-        quantise(0, BATCH - 1)
-        for b in range(IMAGES_PER_HALF, BATCH):
-            quantise(1, b)
-
+        transpose_memory(3)
+        sum_squares(6)
+        invert_norm(5)
+        spread_norm(5)
+        normalise(5)
+        sum_squares(7)
+        invert_norm(6)
+        spread_norm(6)
+        normalise(6)
+        quantise(0, 2)
+        invert_norm(7)
+        spread_norm(7)
+        for b in range(2, BATCH):
+            group_memory(nc.scalar.copy, b)
+        multiply(0)
+        statistics(0)
+        quantise(1, 2)
+        normalise(7)
+        multiply(1)
+        statistics(1)
+        quantise(1, 3)
+        quantise(0, 3)
         gain_t = psum.tile([P, 2 * HALF], BF16, tag="spread")
         nc.tensor.transpose(gain_t[:, 0:P], gain_rows[:], ident_bf16[:])
-        gamma_and_u = keep.tile([P, 2], F32)
-        nc.vector.tensor_copy(out=gamma_and_u[:, 0:1], in_=gain_t[:, 0:1])
-        minus_gamma = keep.tile([P, 1], F32)
-        nc.vector.tensor_scalar_mul(out=minus_gamma[:], in0=gain_t[:, 0:1], scalar1=-1.0)
-        zero_and_beta = keep.tile([P, 2], F32)
-        nc.vector.memset(zero_and_beta[:, 0:1], 0.0)
-        nc.vector.tensor_copy(out=zero_and_beta[:, 1:2], in_=gain_t[:, 1:2])
-
-        for h in range(HALVES):
-            y_bank = psum.tile([P, HALF], F32, tag="x_t_then_y", name="y_bank%d" % h)
-            y_banks.append(y_bank)
-            multiply(0, h, True, False)
-            multiply(1, h, False, True)
-            nc.vector.bn_stats(out=stats[:, h, :], in_=y_banks[h][:])
+        nc.scalar.copy(out=gamma_and_u[:, 0:1], in_=gain_t[:, 0:1])
+        nc.scalar.mul(out=minus_gamma[:], in_=gain_t[:, 0:1], mul=-1.0)
+        nc.scalar.copy(out=zero_and_beta[:, 1:2], in_=gain_t[:, 1:2])
+        multiply(2)
+        multiply(3)
+        statistics(2)
+        statistics(3)
 
         mean_var = keep.tile([P, 2], F32)
-        nc.vector.bn_aggr(out=mean_var[:], in_=stats[:].rearrange("p h s -> p (h s)"))
+        nc.vector.bn_aggr(out=mean_var[:], in_=stats[:])
         inv_std = keep.tile([P, 1], F32)
         nc.scalar.activation(out=inv_std[:], in_=mean_var[:, 1:2], func=ACT.Abs_reciprocal_sqrt, bias=BN_EPS)
         nc.vector.tensor_scalar_mul(out=gamma_and_u[:, 1:2], in0=mean_var[:, 0:1], scalar1=minus_gamma[:])
@@ -221,29 +282,28 @@ def tile_memory_sup_pb_s_kernel(
         )
         scale = scale_shift[:, 0:1]
         shift = scale_shift[:, 1:2]
-        result = keep.tile([P, HALVES, HALF], F32)
+        result = keep.tile([P, BATCH, PIXELS], F32)
 
-        def in_pixel_order(bank):
-            return bank.rearrange("o (b e q) -> o b q e", b=IMAGES_PER_HALF, e=2)
+        def in_pixel_order(b):
+            return y_banks[b][:].rearrange("o (e q) -> o q e", e=2)
 
-        def as_written(bank):
-            return bank.rearrange("o (b q e) -> o b q e", b=IMAGES_PER_HALF, e=2)
+        def as_written(b):
+            return result[:, b, :].rearrange("o (q e) -> o q e", e=2)
 
-        nc.scalar.activation(
-            out=as_written(result[:, 0, :]), in_=in_pixel_order(y_banks[0][:]), func=ACT.Relu, bias=shift, scale=scale
-        )
+        out_view = out.rearrange("b o h w -> b o (h w)")
+        nc.scalar.activation(out=as_written(0), in_=in_pixel_order(0), func=ACT.Relu, bias=shift, scale=scale)
+        nc.sync.dma_start(out=out_view[0], in_=result[:, 0, :])
         nc.vector.tensor_scalar(
-            out=as_written(result[:, 1, :]),
-            in0=in_pixel_order(y_banks[1][:]),
+            out=as_written(3),
+            in0=in_pixel_order(3),
             scalar1=scale,
             scalar2=shift,
             op0=ALU.mult,
             op1=ALU.add,
         )
-        nc.vector.tensor_scalar_max(out=result[:, 1, :], in0=result[:, 1, :], scalar1=0.0)
-        out_view = out.rearrange("b o h w -> o b (h w)")
-        for h in range(HALVES):
-            nc.sync.dma_start(
-                out=out_view[:, h * IMAGES_PER_HALF : (h + 1) * IMAGES_PER_HALF, :],
-                in_=result[:, h, :].rearrange("o (b n) -> o b n", b=IMAGES_PER_HALF),
-            )
+        nc.vector.tensor_scalar_max(out=result[:, 3, :], in0=result[:, 3, :], scalar1=0.0)
+        nc.scalar.activation(out=as_written(1), in_=in_pixel_order(1), func=ACT.Relu, bias=shift, scale=scale)
+        nc.sync.dma_start(out=out_view[3], in_=result[:, 3, :])
+        nc.sync.dma_start(out=out_view[1], in_=result[:, 1, :])
+        nc.scalar.activation(out=as_written(2), in_=in_pixel_order(2), func=ACT.Relu, bias=shift, scale=scale)
+        nc.sync.dma_start(out=out_view[2], in_=result[:, 2, :])

@@ -19,9 +19,11 @@ BATCH = 4
 CHANNELS = 512
 PIXELS = 256
 PAIRS = PIXELS // 2
+HALF = PIXELS // 2
+QUARTER = HALF // 2
 ROWS = BATCH * PIXELS
 OUT_CH = 128
-HALF = 512
+BANK = 512
 PLANES = BATCH * 2
 SCALAR_STATS = 2
 L2_EPS = 1e-12
@@ -90,7 +92,7 @@ def tile_memory_sup_pb_s_kernel(
         grouped = keep.tile([P, 2, ROWS, PACK], BF16, align_bytes=64)
         codes = keep.tile([P, 2, ROWS], U32, align_bytes=64)
         scales = keep.tile([P, 2, ROWS], U8, align_bytes=64)
-        stats = keep.tile([P, SCALAR_STATS * 3 + (BATCH - SCALAR_STATS) * 6], F32)
+        stats = keep.tile([P, SCALAR_STATS * 3 + (BATCH - SCALAR_STATS) * 12], F32)
         nc.vector.memset(stats[:, 0 : 3 * SCALAR_STATS], float(PIXELS))
         unread = keep.tile([P, SCALAR_STATS, 2, PIXELS], F32)
         gamma_and_u = keep.tile([P, 2], F32)
@@ -125,152 +127,172 @@ def tile_memory_sup_pb_s_kernel(
             nc.scalar.activation(out=inv_norm[:, column], in_=sumsq[:, column], func=ACT.Abs_reciprocal_sqrt)
 
         def spread_norm(plane):
-            spread = psum.tile([P, HALF], F32, tag="spread")
+            spread = psum.tile([P, BANK], F32, tag="spread")
             nc.tensor.transpose(
                 spread[:, 0:PAIRS], inv_norm[:, plane : plane + 1].to_broadcast([P, P]), ident_f32[:]
             )
             spread_banks[plane] = spread
 
-        def normalise(plane):
+        def normalise(plane, halves=slice(0, 2)):
             b, e = divmod(plane, 2)
+            count = halves.stop - halves.start
             nc.vector.scalar_tensor_tensor(
-                out=grouped[:, 0, plane * PAIRS : (plane + 1) * PAIRS, :],
-                in0=spread_banks[plane][:, 0:PAIRS].unsqueeze(2).to_broadcast([P, PAIRS, PACK]),
+                out=grouped[:, 0, b * PIXELS : (b + 1) * PIXELS, :].rearrange(
+                    "p (h e q) t -> p e h q t", h=2, e=2
+                )[:, e, halves],
+                in0=spread_banks[plane][:, 0:PAIRS]
+                .rearrange("p (h q) -> p h q", h=2)[:, halves]
+                .unsqueeze(3)
+                .to_broadcast([P, count, QUARTER, PACK]),
                 scalar=1.0 / L2_EPS,
-                in1=x_sb[:, b].rearrange("p t (q e) -> p e q t", e=2)[:, e],
+                in1=x_sb[:, b].rearrange("p t (h q e) -> p e h q t", h=2, e=2)[:, e, halves],
                 op0=ALU.min,
                 op1=ALU.mult,
             )
 
         def transpose_memory(b):
-            m_t = psum.tile([P, 2, 2, PAIRS], F32, tag="m_t_then_y", name="m_t%d" % b, bufs=BATCH)
+            m_t = psum.tile([P, 2, 2, 2, QUARTER], F32, tag="m_t_then_y", name="m_t%d" % b, bufs=BATCH)
             for e in range(2):
                 words = mem_sb[:, b, e, :].bitcast(F32)
                 for u in range(2):
-                    nc.tensor.transpose(m_t[:, e, u, :], words[:, u : CHANNELS // 2 : 2], ident_f32[:])
+                    nc.tensor.transpose(m_t[:, u, :, e, :], words[:, u : CHANNELS // 2 : 2], ident_f32[:])
             mem_banks[b] = m_t
 
         def group_memory(copy, b):
             copy(
-                out=grouped[:, 1, b * PIXELS : (b + 1) * PIXELS, :]
+                out=grouped[:, 1, b * PIXELS : (b + 1) * PIXELS, :].rearrange("p n t -> p (n t)")
                 .bitcast(F32)
-                .rearrange("p (e q) u -> p e q u", e=2),
-                in_=mem_banks[b][:].rearrange("p e u q -> p e q u"),
+                .rearrange("p (n u) -> p n u", u=2),
+                in_=mem_banks[b][:].rearrange("p u h e q -> p (h e q) u"),
             )
 
-        def quantise(g, b):
-            cols = slice(b * PIXELS, (b + 1) * PIXELS)
+        def quantise(g, b, halves=slice(0, 2)):
+            cols = slice(b * PIXELS + halves.start * HALF, b * PIXELS + halves.stop * HALF)
             nc.vector.quantize_mx(
                 out=codes[:, g, cols].bitcast(FP8X4),
                 scales=scales[:, g, cols],
                 in_=grouped[:, g, cols, :].rearrange("p n t -> p (n t)"),
             )
 
-        def multiply(b):
-            y_bank = psum.tile([P, PIXELS], F32, tag="m_t_then_y", name="y_bank%d" % b, bufs=BATCH)
-            y_banks.append(y_bank)
-            for e in range(2):
-                cols = slice((2 * b + e) * PAIRS, (2 * b + e + 1) * PAIRS)
-                for g in (1, 0):
-                    nc.tensor.matmul_mx(
-                        out=y_bank[:, e * PAIRS : (e + 1) * PAIRS],
-                        lhsT=w_words[:, g, :].bitcast(FP4X4),
-                        lhsT_scale=w_scales[:, g, :],
-                        rhs=codes[:, g, cols].bitcast(FP8X4),
-                        rhs_scale=scales[:, g, cols],
-                        start=(g == 1),
-                        stop=(g == 0),
-                    )
+        def new_bank(tag, b, h):
+            return psum.tile([P, PIXELS], F32, tag=tag, name="y_bank%d_%d" % (b, h), bufs=BATCH if tag == "m_t_then_y" else 2)
 
-        def statistics(b):
-            if b < SCALAR_STATS:
-                mean = stats[:, 3 * b + 1 : 3 * b + 2]
-                nc.scalar.activation(
-                    out=unread[:, b, 0, :], in_=y_banks[b][:], func=ACT.Identity, scale=1.0 / PIXELS, accum_out=mean
+        def multiply(b, h, y):
+            cols = slice(b * PIXELS + h * HALF, b * PIXELS + (h + 1) * HALF)
+            for g in (1, 0):
+                nc.tensor.matmul_mx(
+                    out=y,
+                    lhsT=w_words[:, g, :].bitcast(FP4X4),
+                    lhsT_scale=w_scales[:, g, :],
+                    rhs=codes[:, g, cols].bitcast(FP8X4),
+                    rhs_scale=scales[:, g, cols],
+                    start=(g == 1),
+                    stop=(g == 0),
                 )
-                nc.scalar.activation(
-                    out=unread[:, b, 1, :],
-                    in_=y_banks[b][:],
-                    func=ACT.Square,
-                    scale=-1.0,
-                    bias=mean,
-                    accum_out=stats[:, 3 * b + 2 : 3 * b + 3],
-                )
-            else:
-                first = 3 * SCALAR_STATS + 6 * (b - SCALAR_STATS)
-                nc.vector.bn_stats(out=stats[:, first : first + 6], in_=y_banks[b][:])
+
+        def scalar_statistics(b, y):
+            mean = stats[:, 3 * b + 1 : 3 * b + 2]
+            nc.scalar.activation(
+                out=unread[:, b, 0, :], in_=y, func=ACT.Identity, scale=1.0 / PIXELS, accum_out=mean
+            )
+            nc.scalar.activation(
+                out=unread[:, b, 1, :],
+                in_=y,
+                func=ACT.Square,
+                scale=-1.0,
+                bias=mean,
+                accum_out=stats[:, 3 * b + 2 : 3 * b + 3],
+            )
+
+        def vector_statistics(b, h, y):
+            first = 3 * SCALAR_STATS + 6 * (2 * (b - SCALAR_STATS) + h)
+            nc.vector.bn_stats(out=stats[:, first : first + 6], in_=y)
 
         transpose_query(0)
         sum_squares(0)
         invert_norm(0)
         transpose_memory(0)
         group_memory(nc.vector.tensor_copy, 0)
-        quantise(1, 0)
         transpose_query(1)
         spread_norm(0)
         normalise(0)
+        quantise(1, 0)
         sum_squares(1)
         invert_norm(1)
         transpose_memory(1)
         spread_norm(1)
         normalise(1)
-        group_memory(nc.vector.tensor_copy, 1)
         transpose_query(2)
         sum_squares(2)
-        sum_squares(3)
         invert_norm(2)
         spread_norm(2)
         normalise(2)
         quantise(0, 0)
-        transpose_query(3)
-        sum_squares(4)
+        sum_squares(3)
         invert_norm(3)
         spread_norm(3)
+        transpose_query(3)
         normalise(3)
-        transpose_memory(2)
-        sum_squares(5)
+        sum_squares(4)
         invert_norm(4)
         spread_norm(4)
         normalise(4)
         quantise(0, 1)
-        quantise(1, 1)
-        transpose_memory(3)
-        sum_squares(6)
+        transpose_memory(2)
+        sum_squares(5)
         invert_norm(5)
         spread_norm(5)
         normalise(5)
-        sum_squares(7)
+        transpose_memory(3)
+        sum_squares(6)
         invert_norm(6)
         spread_norm(6)
         normalise(6)
         quantise(0, 2)
+        sum_squares(7)
         invert_norm(7)
         spread_norm(7)
-        for b in range(2, BATCH):
-            group_memory(nc.scalar.copy, b)
-        multiply(0)
-        statistics(0)
-        quantise(1, 2)
+        group_memory(nc.scalar.copy, 1)
+        quantise(1, 1)
+        group_memory(nc.scalar.copy, 2)
+        group_memory(nc.scalar.copy, 3)
         normalise(7)
-        multiply(1)
-        statistics(1)
-        quantise(1, 3)
-        quantise(0, 3)
-        gain_t = psum.tile([P, 2 * HALF], BF16, tag="spread")
+        gain_t = psum.tile([P, 2 * BANK], BF16, tag="spread")
         nc.tensor.transpose(gain_t[:, 0:P], gain_rows[:], ident_bf16[:])
         nc.scalar.copy(out=gamma_and_u[:, 0:1], in_=gain_t[:, 0:1])
         nc.scalar.mul(out=minus_gamma[:], in_=gain_t[:, 0:1], mul=-1.0)
         nc.scalar.copy(out=zero_and_beta[:, 1:2], in_=gain_t[:, 1:2])
-        multiply(2)
-        multiply(3)
-        statistics(2)
-        statistics(3)
+        y = {}
+        y[0] = new_bank("m_t_then_y", 0, 0)
+        multiply(0, 0, y[0][:, 0:HALF])
+        multiply(0, 1, y[0][:, HALF:PIXELS])
+        scalar_statistics(0, y[0][:])
+        y[1] = new_bank("m_t_then_y", 1, 0)
+        multiply(1, 0, y[1][:, 0:HALF])
+        multiply(1, 1, y[1][:, HALF:PIXELS])
+        quantise(1, 2)
+        quantise(0, 3)
+        y[2, 0] = new_bank("m_t_then_y", 2, 0)
+        multiply(2, 0, y[2, 0][:, 0:HALF])
+        y[2, 1] = new_bank("m_t_then_y", 2, 1)
+        multiply(2, 1, y[2, 1][:, 0:HALF])
+        scalar_statistics(1, y[1][:])
+        quantise(1, 3, slice(0, 1))
+        quantise(1, 3, slice(1, 2))
+        vector_statistics(2, 0, y[2, 0][:, 0:HALF])
+        vector_statistics(2, 1, y[2, 1][:, 0:HALF])
+        y[3, 0] = new_bank("x_t", 3, 0)
+        multiply(3, 0, y[3, 0][:, 0:HALF])
+        y[3, 1] = new_bank("x_t", 3, 1)
+        multiply(3, 1, y[3, 1][:, 0:HALF])
+        vector_statistics(3, 0, y[3, 0][:, 0:HALF])
+        vector_statistics(3, 1, y[3, 1][:, 0:HALF])
 
         mean_var = keep.tile([P, 2], F32)
         nc.vector.bn_aggr(out=mean_var[:], in_=stats[:])
         inv_std = keep.tile([P, 1], F32)
         nc.scalar.activation(out=inv_std[:], in_=mean_var[:, 1:2], func=ACT.Abs_reciprocal_sqrt, bias=BN_EPS)
-        nc.vector.tensor_scalar_mul(out=gamma_and_u[:, 1:2], in0=mean_var[:, 0:1], scalar1=minus_gamma[:])
+        nc.vector.tensor_tensor(out=gamma_and_u[:, 1:2], in0=mean_var[:, 0:1], in1=minus_gamma[:], op=ALU.mult)
         scale_shift = keep.tile([P, 2], F32)
         nc.vector.scalar_tensor_tensor(
             out=scale_shift[:],
@@ -283,27 +305,43 @@ def tile_memory_sup_pb_s_kernel(
         scale = scale_shift[:, 0:1]
         shift = scale_shift[:, 1:2]
         result = keep.tile([P, BATCH, PIXELS], F32)
-
-        def in_pixel_order(b):
-            return y_banks[b][:].rearrange("o (e q) -> o q e", e=2)
-
-        def as_written(b):
-            return result[:, b, :].rearrange("o (q e) -> o q e", e=2)
-
         out_view = out.rearrange("b o h w -> b o (h w)")
-        nc.scalar.activation(out=as_written(0), in_=in_pixel_order(0), func=ACT.Relu, bias=shift, scale=scale)
-        nc.sync.dma_start(out=out_view[0], in_=result[:, 0, :])
-        nc.vector.tensor_scalar(
-            out=as_written(3),
-            in0=in_pixel_order(3),
-            scalar1=scale,
-            scalar2=shift,
-            op0=ALU.mult,
-            op1=ALU.add,
-        )
-        nc.vector.tensor_scalar_max(out=result[:, 3, :], in0=result[:, 3, :], scalar1=0.0)
-        nc.scalar.activation(out=as_written(1), in_=in_pixel_order(1), func=ACT.Relu, bias=shift, scale=scale)
-        nc.sync.dma_start(out=out_view[3], in_=result[:, 3, :])
-        nc.sync.dma_start(out=out_view[1], in_=result[:, 1, :])
-        nc.scalar.activation(out=as_written(2), in_=in_pixel_order(2), func=ACT.Relu, bias=shift, scale=scale)
-        nc.sync.dma_start(out=out_view[2], in_=result[:, 2, :])
+
+        def store(b, pixels):
+            nc.sync.dma_start(out=out_view[b, :, pixels], in_=result[:, b, pixels])
+
+        def by_pixels(y):
+            return y.rearrange("o (h e q) -> o h q e", e=2, q=QUARTER)
+
+        def in_order(b, pixels):
+            return result[:, b, pixels].rearrange("o (h q e) -> o h q e", e=2, q=QUARTER)
+
+        def scalar_finish(b, pixels, y):
+            nc.scalar.activation(
+                out=in_order(b, pixels), in_=by_pixels(y), func=ACT.Relu, bias=shift, scale=scale
+            )
+            store(b, pixels)
+
+        def vector_affine(b, pixels, y):
+            nc.vector.scalar_tensor_tensor(
+                out=result[:, b, pixels].rearrange("o (q e) -> o q e", e=2),
+                in0=y.rearrange("o (e q) -> o q e", e=2),
+                scalar=scale,
+                in1=shift.unsqueeze(2).to_broadcast([P, QUARTER, 2]),
+                op0=ALU.mult,
+                op1=ALU.add,
+            )
+
+        def vector_relu(b, pixels):
+            nc.vector.tensor_scalar_max(out=result[:, b, pixels], in0=result[:, b, pixels], scalar1=0.0)
+            store(b, pixels)
+
+        half = (slice(0, HALF), slice(HALF, PIXELS))
+        whole = slice(0, PIXELS)
+        scalar_finish(2, half[0], y[2, 0][:, 0:HALF])
+        vector_affine(3, half[0], y[3, 0][:, 0:HALF])
+        scalar_finish(2, half[1], y[2, 1][:, 0:HALF])
+        vector_affine(3, half[1], y[3, 1][:, 0:HALF])
+        vector_relu(3, whole)
+        scalar_finish(0, whole, y[0][:])
+        scalar_finish(1, whole, y[1][:])

@@ -89,6 +89,8 @@ def tile_memory_sup_pb_s_kernel(
         sumsq = keep.tile([P, PLANES], F32)
         squares = keep.tile([P, PLANES, CHANNELS], BF16)
         inv_norm = keep.tile([P, PLANES], F32)
+        guarded = keep.tile([P, PLANES], F32)
+        q_rows = keep.tile([P, CHANNELS], BF16)
         grouped = keep.tile([P, 2, ROWS, PACK], BF16, align_bytes=64)
         codes = keep.tile([P, 2, ROWS], U32, align_bytes=64)
         scales = keep.tile([P, 2, ROWS], U8, align_bytes=64)
@@ -133,6 +135,45 @@ def tile_memory_sup_pb_s_kernel(
             )
             spread_banks[plane] = spread
 
+        def guard(plane):
+            column = slice(plane, plane + 1)
+            nc.scalar.activation(out=guarded[:, column], in_=sumsq[:, column], func=ACT.Relu, bias=-L2_EPS * L2_EPS)
+
+        def invert_guarded(plane):
+            column = slice(plane, plane + 1)
+            nc.scalar.activation(
+                out=inv_norm[:, column],
+                in_=guarded[:, column],
+                func=ACT.Abs_reciprocal_sqrt,
+                bias=L2_EPS * L2_EPS,
+            )
+
+        def scalar_normalise(plane):
+            b, e = divmod(plane, 2)
+            pixel_pairs = query_banks[b][:].rearrange("q t p -> q (t p)").bitcast(BF16)
+            nc.scalar.activation(
+                out=q_rows[:].rearrange("q (p t) -> q p t", t=PACK),
+                in_=pixel_pairs.rearrange("q (t p e) -> q e p t", t=PACK, e=2)[:, e],
+                func=ACT.Copy,
+                scale=inv_norm[:, plane : plane + 1],
+            )
+
+        def transpose_back(plane):
+            q_t = psum.tile([P, 2, PAIRS], F32, tag="x_t")
+            words = q_rows[:].bitcast(F32)
+            for u in range(2):
+                nc.tensor.transpose(q_t[:, u, :], words[:, u : CHANNELS // 2 : 2], ident_f32[:])
+            spread_banks[plane] = q_t
+
+        def group_query(plane):
+            b, e = divmod(plane, 2)
+            nc.scalar.copy(
+                out=grouped[:, 0, b * PIXELS : (b + 1) * PIXELS, :].rearrange("p n t -> p (n t)")
+                .bitcast(F32)
+                .rearrange("p (h e q u) -> p e h q u", h=2, e=2, u=2)[:, e],
+                in_=spread_banks[plane][:].rearrange("p u (h q) -> p h q u", h=2),
+            )
+
         def normalise(plane, halves=slice(0, 2)):
             b, e = divmod(plane, 2)
             count = halves.stop - halves.start
@@ -166,6 +207,33 @@ def tile_memory_sup_pb_s_kernel(
                 in_=mem_banks[b][:].rearrange("p u h e q -> p (h e q) u"),
             )
 
+        def vector_memory_half(b, h):
+            first = b * PIXELS + h * HALF
+            nc.vector.tensor_copy(
+                out=grouped[:, 1, first : first + HALF, :].rearrange("p n t -> p (n t)")
+                .bitcast(F32)
+                .rearrange("p (n u) -> p n u", u=2),
+                in_=mem_banks[b][:, :, h].rearrange("p u e q -> p (e q) u"),
+            )
+
+        def scalar_memory_half(b, h):
+            first = b * PIXELS + h * HALF
+            nc.scalar.copy(
+                out=grouped[:, 1, first : first + HALF, :].rearrange("p n t -> p (n t)")
+                .bitcast(F32)
+                .rearrange("p (n u) -> p n u", u=2),
+                in_=mem_banks[b][:, :, h].rearrange("p u e q -> p (e q) u"),
+            )
+
+        def group_memory_quarter(b, h, e):
+            first = b * PIXELS + h * HALF + e * QUARTER
+            nc.scalar.copy(
+                out=grouped[:, 1, first : first + QUARTER, :].rearrange("p n t -> p (n t)")
+                .bitcast(F32)
+                .rearrange("p (n u) -> p n u", u=2),
+                in_=mem_banks[b][:, :, h, e, :].rearrange("p u q -> p q u"),
+            )
+
         def quantise(g, b, halves=slice(0, 2)):
             cols = slice(b * PIXELS + halves.start * HALF, b * PIXELS + halves.stop * HALF)
             nc.vector.quantize_mx(
@@ -190,17 +258,22 @@ def tile_memory_sup_pb_s_kernel(
                     stop=(g == 0),
                 )
 
-        def scalar_statistics(b, y):
-            mean = stats[:, 3 * b + 1 : 3 * b + 2]
+        def scalar_mean(b, y):
             nc.scalar.activation(
-                out=unread[:, b, 0, :], in_=y, func=ACT.Identity, scale=1.0 / PIXELS, accum_out=mean
+                out=unread[:, b, 0, :],
+                in_=y,
+                func=ACT.Identity,
+                scale=1.0 / PIXELS,
+                accum_out=stats[:, 3 * b + 1 : 3 * b + 2],
             )
+
+        def scalar_variance(b, y):
             nc.scalar.activation(
                 out=unread[:, b, 1, :],
                 in_=y,
                 func=ACT.Square,
                 scale=-1.0,
-                bias=mean,
+                bias=stats[:, 3 * b + 1 : 3 * b + 2],
                 accum_out=stats[:, 3 * b + 2 : 3 * b + 3],
             )
 
@@ -213,50 +286,55 @@ def tile_memory_sup_pb_s_kernel(
         invert_norm(0)
         transpose_memory(0)
         group_memory(nc.vector.tensor_copy, 0)
+        quantise(1, 0)
         transpose_query(1)
         spread_norm(0)
         normalise(0)
-        quantise(1, 0)
         sum_squares(1)
-        invert_norm(1)
         transpose_memory(1)
-        spread_norm(1)
-        normalise(1)
+        group_memory(nc.vector.tensor_copy, 1)
         transpose_query(2)
         sum_squares(2)
+        invert_norm(1)
+        spread_norm(1)
+        normalise(1)
+        sum_squares(3)
         invert_norm(2)
         spread_norm(2)
         normalise(2)
         quantise(0, 0)
-        sum_squares(3)
+        transpose_query(3)
+        sum_squares(4)
         invert_norm(3)
         spread_norm(3)
-        transpose_query(3)
         normalise(3)
-        sum_squares(4)
+        transpose_memory(2)
+        sum_squares(5)
         invert_norm(4)
         spread_norm(4)
         normalise(4)
         quantise(0, 1)
-        transpose_memory(2)
-        sum_squares(5)
-        invert_norm(5)
-        spread_norm(5)
-        normalise(5)
-        transpose_memory(3)
+        quantise(1, 1)
         sum_squares(6)
+        guard(5)
+        scalar_memory_half(2, 0)
         invert_norm(6)
+        invert_guarded(5)
+        transpose_memory(3)
         spread_norm(6)
         normalise(6)
-        quantise(0, 2)
         sum_squares(7)
+        scalar_memory_half(2, 1)
         invert_norm(7)
         spread_norm(7)
-        group_memory(nc.scalar.copy, 1)
-        quantise(1, 1)
-        group_memory(nc.scalar.copy, 2)
-        group_memory(nc.scalar.copy, 3)
+        quantise(1, 2)
         normalise(7)
+        scalar_normalise(5)
+        transpose_back(5)
+        scalar_memory_half(3, 0)
+        scalar_memory_half(3, 1)
+        quantise(0, 3)
+        group_query(5)
         gain_t = psum.tile([P, 2 * BANK], BF16, tag="spread")
         nc.tensor.transpose(gain_t[:, 0:P], gain_rows[:], ident_bf16[:])
         nc.scalar.copy(out=gamma_and_u[:, 0:1], in_=gain_t[:, 0:1])
@@ -266,27 +344,28 @@ def tile_memory_sup_pb_s_kernel(
         y[0] = new_bank("m_t_then_y", 0, 0)
         multiply(0, 0, y[0][:, 0:HALF])
         multiply(0, 1, y[0][:, HALF:PIXELS])
-        scalar_statistics(0, y[0][:])
+        scalar_mean(0, y[0][:])
         y[1] = new_bank("m_t_then_y", 1, 0)
         multiply(1, 0, y[1][:, 0:HALF])
         multiply(1, 1, y[1][:, HALF:PIXELS])
-        quantise(1, 2)
-        quantise(0, 3)
-        y[2, 0] = new_bank("m_t_then_y", 2, 0)
-        multiply(2, 0, y[2, 0][:, 0:HALF])
-        y[2, 1] = new_bank("m_t_then_y", 2, 1)
-        multiply(2, 1, y[2, 1][:, 0:HALF])
-        scalar_statistics(1, y[1][:])
-        quantise(1, 3, slice(0, 1))
-        quantise(1, 3, slice(1, 2))
-        vector_statistics(2, 0, y[2, 0][:, 0:HALF])
-        vector_statistics(2, 1, y[2, 1][:, 0:HALF])
+        quantise(1, 3)
         y[3, 0] = new_bank("x_t", 3, 0)
         multiply(3, 0, y[3, 0][:, 0:HALF])
         y[3, 1] = new_bank("x_t", 3, 1)
         multiply(3, 1, y[3, 1][:, 0:HALF])
+        quantise(0, 2, slice(0, 1))
+        quantise(0, 2, slice(1, 2))
         vector_statistics(3, 0, y[3, 0][:, 0:HALF])
         vector_statistics(3, 1, y[3, 1][:, 0:HALF])
+        scalar_mean(1, y[1][:])
+        scalar_variance(0, y[0][:])
+        scalar_variance(1, y[1][:])
+        y[2, 0] = new_bank("m_t_then_y", 2, 0)
+        multiply(2, 0, y[2, 0][:, 0:HALF])
+        y[2, 1] = new_bank("m_t_then_y", 2, 1)
+        multiply(2, 1, y[2, 1][:, 0:HALF])
+        vector_statistics(2, 0, y[2, 0][:, 0:HALF])
+        vector_statistics(2, 1, y[2, 1][:, 0:HALF])
 
         mean_var = keep.tile([P, 2], F32)
         nc.vector.bn_aggr(out=mean_var[:], in_=stats[:])

@@ -69,9 +69,14 @@ def tile_memory_sup_pb_s_kernel(
         def load_memory(b):
             nc.sync.dma_start(out=mem_sb[:, b], in_=mem_view[:, b])
 
-        for b in range(BATCH):
-            load_image(b, pieces=2 if b == 0 else 1)
-            load_memory(b)
+        load_image(0, pieces=2)
+        load_memory(0)
+        load_image(1, pieces=1)
+        load_memory(1)
+        load_image(2, pieces=1)
+        load_image(3, pieces=1)
+        load_memory(2)
+        load_memory(3)
         w_words = keep.tile([P, 2, 2 * OUT_CH], U8, align_bytes=64)
         nc.sync.dma_start(
             out=w_words[:].bitcast(I32), in_=conv_w_words.rearrange("g p n -> p g n").bitcast(I32)
@@ -245,18 +250,17 @@ def tile_memory_sup_pb_s_kernel(
         def new_bank(tag, b, h):
             return psum.tile([P, PIXELS], F32, tag=tag, name="y_bank%d_%d" % (b, h), bufs=BATCH if tag == "m_t_then_y" else 2)
 
-        def multiply(b, h, y):
+        def multiply(b, h, g, y, start):
             cols = slice(b * PIXELS + h * HALF, b * PIXELS + (h + 1) * HALF)
-            for g in (1, 0):
-                nc.tensor.matmul_mx(
-                    out=y,
-                    lhsT=w_words[:, g, :].bitcast(FP4X4),
-                    lhsT_scale=w_scales[:, g, :],
-                    rhs=codes[:, g, cols].bitcast(FP8X4),
-                    rhs_scale=scales[:, g, cols],
-                    start=(g == 1),
-                    stop=(g == 0),
-                )
+            nc.tensor.matmul_mx(
+                out=y,
+                lhsT=w_words[:, g, :].bitcast(FP4X4),
+                lhsT_scale=w_scales[:, g, :],
+                rhs=codes[:, g, cols].bitcast(FP8X4),
+                rhs_scale=scales[:, g, cols],
+                start=start,
+                stop=not start,
+            )
 
         def scalar_mean(b, y):
             nc.scalar.activation(
@@ -329,41 +333,47 @@ def tile_memory_sup_pb_s_kernel(
         spread_norm(7)
         quantise(1, 2)
         normalise(7)
+        y = {}
+        y[0] = new_bank("m_t_then_y", 0, 0)
+        for h in range(2):
+            multiply(0, h, 1, y[0][:, h * HALF : (h + 1) * HALF], True)
+            multiply(0, h, 0, y[0][:, h * HALF : (h + 1) * HALF], False)
         scalar_normalise(5)
         transpose_back(5)
         scalar_memory_half(3, 0)
         scalar_memory_half(3, 1)
-        quantise(0, 3)
+        scalar_mean(0, y[0][:])
+        quantise(1, 3)
         group_query(5)
         gain_t = psum.tile([P, 2 * BANK], BF16, tag="spread")
         nc.tensor.transpose(gain_t[:, 0:P], gain_rows[:], ident_bf16[:])
         nc.scalar.copy(out=gamma_and_u[:, 0:1], in_=gain_t[:, 0:1])
         nc.scalar.mul(out=minus_gamma[:], in_=gain_t[:, 0:1], mul=-1.0)
         nc.scalar.copy(out=zero_and_beta[:, 1:2], in_=gain_t[:, 1:2])
-        y = {}
-        y[0] = new_bank("m_t_then_y", 0, 0)
-        multiply(0, 0, y[0][:, 0:HALF])
-        multiply(0, 1, y[0][:, HALF:PIXELS])
-        scalar_mean(0, y[0][:])
         y[1] = new_bank("m_t_then_y", 1, 0)
-        multiply(1, 0, y[1][:, 0:HALF])
-        multiply(1, 1, y[1][:, HALF:PIXELS])
-        quantise(1, 3)
+        for h in range(2):
+            multiply(1, h, 1, y[1][:, h * HALF : (h + 1) * HALF], True)
+            multiply(1, h, 0, y[1][:, h * HALF : (h + 1) * HALF], False)
+        y[2, 0] = new_bank("m_t_then_y", 2, 0)
+        multiply(2, 0, 1, y[2, 0][:, 0:HALF], True)
+        y[2, 1] = new_bank("m_t_then_y", 2, 1)
+        multiply(2, 1, 1, y[2, 1][:, 0:HALF], True)
         y[3, 0] = new_bank("x_t", 3, 0)
-        multiply(3, 0, y[3, 0][:, 0:HALF])
+        multiply(3, 0, 1, y[3, 0][:, 0:HALF], True)
         y[3, 1] = new_bank("x_t", 3, 1)
-        multiply(3, 1, y[3, 1][:, 0:HALF])
+        multiply(3, 1, 1, y[3, 1][:, 0:HALF], True)
+        quantise(0, 3)
         quantise(0, 2, slice(0, 1))
         quantise(0, 2, slice(1, 2))
-        vector_statistics(3, 0, y[3, 0][:, 0:HALF])
-        vector_statistics(3, 1, y[3, 1][:, 0:HALF])
+        multiply(3, 0, 0, y[3, 0][:, 0:HALF], False)
+        multiply(3, 1, 0, y[3, 1][:, 0:HALF], False)
         scalar_mean(1, y[1][:])
         scalar_variance(0, y[0][:])
         scalar_variance(1, y[1][:])
-        y[2, 0] = new_bank("m_t_then_y", 2, 0)
-        multiply(2, 0, y[2, 0][:, 0:HALF])
-        y[2, 1] = new_bank("m_t_then_y", 2, 1)
-        multiply(2, 1, y[2, 1][:, 0:HALF])
+        multiply(2, 0, 0, y[2, 0][:, 0:HALF], False)
+        multiply(2, 1, 0, y[2, 1][:, 0:HALF], False)
+        vector_statistics(3, 0, y[3, 0][:, 0:HALF])
+        vector_statistics(3, 1, y[3, 1][:, 0:HALF])
         vector_statistics(2, 0, y[2, 0][:, 0:HALF])
         vector_statistics(2, 1, y[2, 1][:, 0:HALF])
 

@@ -43,13 +43,9 @@ def tile_memory_sup_pb_s_kernel(
 
         ident_f32 = keep.tile([P, P], F32)
         make_identity(nc, ident_f32[:])
-        ident_bf16 = keep.tile([P, P], BF16)
-        make_identity(nc, ident_bf16[:])
 
         one = keep.tile([P, 1], F32)
         nc.vector.memset(one[:], 1.0)
-        gain_rows = keep.tile([P, P], BF16)
-        nc.vector.memset(gain_rows[:], 0.0)
         w_scales = keep.tile([P, 2, OUT_CH], U8, align_bytes=64)
         nc.vector.memset(w_scales[:].rearrange("p g n -> p (g n)").bitcast(I32), 0)
 
@@ -66,11 +62,13 @@ def tile_memory_sup_pb_s_kernel(
             for t in range(0, PACK, step):
                 nc.sync.dma_start(out=x_sb[:, b, t : t + step], in_=channels[:, t : t + step])
 
-        def load_memory(b):
-            nc.sync.dma_start(out=mem_sb[:, b], in_=mem_view[:, b])
+        def load_memory(b, pieces=1):
+            step = 2 // pieces
+            for e in range(0, 2, step):
+                nc.sync.dma_start(out=mem_sb[:, b, e : e + step], in_=mem_view[:, b, e : e + step])
 
         load_image(0, pieces=2)
-        load_memory(0)
+        load_memory(0, pieces=2)
         load_image(1, pieces=1)
         load_memory(1)
         load_image(2, pieces=1)
@@ -88,8 +86,10 @@ def tile_memory_sup_pb_s_kernel(
                 .rearrange("g r n -> r g n")
                 .bitcast(I32),
             )
-        nc.sync.dma_start(out=gain_rows[0:1, :], in_=bn_gamma.unsqueeze(0))
-        nc.sync.dma_start(out=gain_rows[1:2, :], in_=bn_beta.unsqueeze(0))
+        gamma = keep.tile([P, 1], BF16)
+        nc.sync.dma_start(out=gamma[:], in_=bn_gamma.unsqueeze(1))
+        beta = keep.tile([P, 1], BF16)
+        nc.sync.dma_start(out=beta[:], in_=bn_beta.unsqueeze(1))
 
         sumsq = keep.tile([P, PLANES], F32)
         squares = keep.tile([P, PLANES, CHANNELS], BF16)
@@ -305,20 +305,20 @@ def tile_memory_sup_pb_s_kernel(
         sum_squares(3)
         invert_norm(2)
         spread_norm(2)
-        normalise(2)
-        quantise(0, 0)
-        transpose_query(3)
-        sum_squares(4)
+        quantise(1, 1)
         invert_norm(3)
+        normalise(2)
+        transpose_query(3)
         spread_norm(3)
+        sum_squares(4)
         normalise(3)
+        quantise(0, 0)
         transpose_memory(2)
         sum_squares(5)
         invert_norm(4)
         spread_norm(4)
         normalise(4)
         quantise(0, 1)
-        quantise(1, 1)
         sum_squares(6)
         guard(5)
         scalar_memory_half(2, 0)
@@ -344,12 +344,6 @@ def tile_memory_sup_pb_s_kernel(
         scalar_memory_half(3, 1)
         scalar_mean(0, y[0][:])
         quantise(1, 3)
-        group_query(5)
-        gain_t = psum.tile([P, 2 * BANK], BF16, tag="spread")
-        nc.tensor.transpose(gain_t[:, 0:P], gain_rows[:], ident_bf16[:])
-        nc.scalar.copy(out=gamma_and_u[:, 0:1], in_=gain_t[:, 0:1])
-        nc.scalar.mul(out=minus_gamma[:], in_=gain_t[:, 0:1], mul=-1.0)
-        nc.scalar.copy(out=zero_and_beta[:, 1:2], in_=gain_t[:, 1:2])
         y[1] = new_bank("m_t_then_y", 1, 0)
         for h in range(2):
             multiply(1, h, 1, y[1][:, h * HALF : (h + 1) * HALF], True)
@@ -360,8 +354,12 @@ def tile_memory_sup_pb_s_kernel(
         multiply(2, 1, 1, y[2, 1][:, 0:HALF], True)
         y[3, 0] = new_bank("x_t", 3, 0)
         multiply(3, 0, 1, y[3, 0][:, 0:HALF], True)
+        group_query(5)
         y[3, 1] = new_bank("x_t", 3, 1)
         multiply(3, 1, 1, y[3, 1][:, 0:HALF], True)
+        nc.scalar.copy(out=gamma_and_u[:, 0:1], in_=gamma[:])
+        nc.scalar.mul(out=minus_gamma[:], in_=gamma[:], mul=-1.0)
+        nc.scalar.copy(out=zero_and_beta[:, 1:2], in_=beta[:])
         quantise(0, 3)
         quantise(0, 2, slice(0, 1))
         quantise(0, 2, slice(1, 2))

@@ -52,8 +52,8 @@ def tile_memory_sup_pb_s_kernel(
         warm = keep.tile([P, 1], F32)
         nc.scalar.activation(out=warm[:], in_=one[:], func=ACT.Abs_reciprocal_sqrt)
 
-        x_sb = keep.tile([P, BATCH, PACK, PIXELS], BF16)
-        mem_sb = keep.tile([P, BATCH, 2, CHANNELS], BF16)
+        x_sb = keep.tile([P, BATCH, PACK, PIXELS], BF16, align_bytes=256)
+        mem_sb = keep.tile([P, BATCH, 2, CHANNELS], BF16, align_bytes=256)
         mem_view = concat_memory.rearrange("(b q e) k -> q b e k", q=PAIRS, e=2)
 
         def load_image(b, pieces):
@@ -96,9 +96,9 @@ def tile_memory_sup_pb_s_kernel(
         inv_norm = keep.tile([P, PLANES], F32)
         guarded = keep.tile([P, PLANES], F32)
         q_rows = keep.tile([P, CHANNELS], BF16)
-        grouped = keep.tile([P, 2, ROWS, PACK], BF16, align_bytes=64)
-        codes = keep.tile([P, 2, ROWS], U32, align_bytes=64)
-        scales = keep.tile([P, 2, ROWS], U8, align_bytes=64)
+        grouped = keep.tile([P, 2, ROWS, PACK], BF16, align_bytes=256)
+        codes = keep.tile([P, 2, ROWS], U32, align_bytes=256)
+        scales = keep.tile([P, 2, ROWS], U8, align_bytes=256)
         stats = keep.tile([P, SCALAR_STATS * 3 + (BATCH - SCALAR_STATS) * 12], F32)
         nc.vector.memset(stats[:, 0 : 3 * SCALAR_STATS], float(PIXELS))
         unread = keep.tile([P, SCALAR_STATS, 2, PIXELS], F32)
@@ -391,7 +391,7 @@ def tile_memory_sup_pb_s_kernel(
         )
         scale = scale_shift[:, 0:1]
         shift = scale_shift[:, 1:2]
-        result = keep.tile([P, BATCH, PIXELS], F32)
+        result = keep.tile([P, BATCH, PIXELS], F32, align_bytes=256)
         out_view = out.rearrange("b o h w -> b o (h w)")
 
         def store(b, pixels):

from contextlib import ExitStack

import concourse.mybir as mybir
from concourse.masks import make_identity

F32 = mybir.dt.float32
BF16 = mybir.dt.bfloat16
I32 = mybir.dt.int32
U32 = mybir.dt.uint32
U8 = mybir.dt.uint8
FP8X4 = mybir.dt.float8_e4m3fn_x4
FP4X4 = mybir.dt.float4_e2m1fn_x4
ACT = mybir.ActivationFunctionType
ALU = mybir.AluOpType

P = 128
PACK = 4
BATCH = 4
CHANNELS = 512
PIXELS = 256
PAIRS = PIXELS // 2
HALF = PIXELS // 2
QUARTER = HALF // 2
ROWS = BATCH * PIXELS
OUT_CH = 128
BANK = 512
PLANES = BATCH * 2
SCALAR_STATS = 2
L2_EPS = 1e-12
BN_EPS = 1e-5

FLOPS = 2 * ROWS * 2 * CHANNELS * OUT_CH


def tile_memory_sup_pb_s_kernel(
    tc, query, concat_memory, conv_w_words, conv_w_scales, bn_gamma, bn_beta, out
):
    nc = tc.nc
    with ExitStack() as ctx:
        keep = ctx.enter_context(tc.tile_pool(name="keep", bufs=1))
        psum = ctx.enter_context(tc.psum_pool(name="psum", bufs=2))
        ctx.enter_context(tc.manual_schedule())

        ident_f32 = keep.tile([P, P], F32)
        make_identity(nc, ident_f32[:])

        one = keep.tile([P, 1], F32)
        nc.vector.memset(one[:], 1.0)
        w_scales = keep.tile([P, 2, OUT_CH], U8, align_bytes=64)
        nc.vector.memset(w_scales[:].rearrange("p g n -> p (g n)").bitcast(I32), 0)

        warm = keep.tile([P, 1], F32)
        nc.scalar.activation(out=warm[:], in_=one[:], func=ACT.Abs_reciprocal_sqrt)

        x_sb = keep.tile([P, BATCH, PACK, PIXELS], BF16, align_bytes=256)
        mem_sb = keep.tile([P, BATCH, 2, CHANNELS], BF16, align_bytes=256)
        mem_view = concat_memory.rearrange("(b q e) k -> q b e k", q=PAIRS, e=2)

        def load_image(b, pieces):
            channels = query[b].rearrange("(p t) h w -> p t (h w)", t=PACK)
            step = PACK // pieces
            for t in range(0, PACK, step):
                nc.sync.dma_start(out=x_sb[:, b, t : t + step], in_=channels[:, t : t + step])

        def load_memory(b, pieces=1):
            step = 2 // pieces
            for e in range(0, 2, step):
                nc.sync.dma_start(out=mem_sb[:, b, e : e + step], in_=mem_view[:, b, e : e + step])

        load_image(0, pieces=2)
        load_memory(0, pieces=2)
        load_image(1, pieces=1)
        load_memory(1)
        load_image(2, pieces=1)
        load_image(3, pieces=1)
        load_memory(2)
        load_memory(3)
        w_words = keep.tile([P, 2, 2 * OUT_CH], U8, align_bytes=64)
        nc.sync.dma_start(
            out=w_words[:].bitcast(I32), in_=conv_w_words.rearrange("g p n -> p g n").bitcast(I32)
        )
        for quadrant in range(4):
            nc.sync.dma_start(
                out=w_scales[32 * quadrant : 32 * quadrant + 4].bitcast(I32),
                in_=conv_w_scales[:, 4 * quadrant : 4 * quadrant + 4, :]
                .rearrange("g r n -> r g n")
                .bitcast(I32),
            )
        gamma = keep.tile([P, 1], BF16)
        nc.sync.dma_start(out=gamma[:], in_=bn_gamma.unsqueeze(1))
        beta = keep.tile([P, 1], BF16)
        nc.sync.dma_start(out=beta[:], in_=bn_beta.unsqueeze(1))

        sumsq = keep.tile([P, PLANES], F32)
        squares = keep.tile([P, PLANES, CHANNELS], BF16)
        inv_norm = keep.tile([P, PLANES], F32)
        guarded = keep.tile([P, PLANES], F32)
        q_rows = keep.tile([P, CHANNELS], BF16)
        grouped = keep.tile([P, 2, ROWS, PACK], BF16, align_bytes=256)
        codes = keep.tile([P, 2, ROWS], U32, align_bytes=256)
        scales = keep.tile([P, 2, ROWS], U8, align_bytes=256)
        stats = keep.tile([P, SCALAR_STATS * 3 + (BATCH - SCALAR_STATS) * 12], F32)
        nc.vector.memset(stats[:, 0 : 3 * SCALAR_STATS], float(PIXELS))
        unread = keep.tile([P, SCALAR_STATS, 2, PIXELS], F32)
        gamma_and_u = keep.tile([P, 2], F32)
        minus_gamma = keep.tile([P, 1], F32)
        zero_and_beta = keep.tile([P, 2], F32)
        nc.vector.memset(zero_and_beta[:, 0:1], 0.0)
        y_banks = []
        mem_banks = {}
        query_banks = []
        spread_banks = {}

        def transpose_query(b):
            x_t = psum.tile([P, PACK, P], F32, tag="x_t")
            for t in range(PACK):
                nc.tensor.transpose(x_t[:, t, :], x_sb[:, b, t, :].bitcast(F32), ident_f32[:])
            query_banks.append(x_t)

        def sum_squares(plane):
            b, e = divmod(plane, 2)
            pixel_pairs = (
                query_banks[b][:].rearrange("q t p -> q (t p)").bitcast(BF16).rearrange("q (c e) -> q c e", e=2)
            )
            nc.scalar.activation(
                out=squares[:, plane, :],
                in_=pixel_pairs[:, :, e],
                func=ACT.Square,
                accum_out=sumsq[:, plane : plane + 1],
            )

        def invert_norm(plane):
            column = slice(plane, plane + 1)
            nc.scalar.activation(out=inv_norm[:, column], in_=sumsq[:, column], func=ACT.Abs_reciprocal_sqrt)

        def spread_norm(plane):
            spread = psum.tile([P, BANK], F32, tag="spread")
            nc.tensor.transpose(
                spread[:, 0:PAIRS], inv_norm[:, plane : plane + 1].to_broadcast([P, P]), ident_f32[:]
            )
            spread_banks[plane] = spread

        def guard(plane):
            column = slice(plane, plane + 1)
            nc.scalar.activation(out=guarded[:, column], in_=sumsq[:, column], func=ACT.Relu, bias=-L2_EPS * L2_EPS)

        def invert_guarded(plane):
            column = slice(plane, plane + 1)
            nc.scalar.activation(
                out=inv_norm[:, column],
                in_=guarded[:, column],
                func=ACT.Abs_reciprocal_sqrt,
                bias=L2_EPS * L2_EPS,
            )

        def scalar_normalise(plane):
            b, e = divmod(plane, 2)
            pixel_pairs = query_banks[b][:].rearrange("q t p -> q (t p)").bitcast(BF16)
            nc.scalar.activation(
                out=q_rows[:].rearrange("q (p t) -> q p t", t=PACK),
                in_=pixel_pairs.rearrange("q (t p e) -> q e p t", t=PACK, e=2)[:, e],
                func=ACT.Copy,
                scale=inv_norm[:, plane : plane + 1],
            )

        def transpose_back(plane):
            q_t = psum.tile([P, 2, PAIRS], F32, tag="x_t")
            words = q_rows[:].bitcast(F32)
            for u in range(2):
                nc.tensor.transpose(q_t[:, u, :], words[:, u : CHANNELS // 2 : 2], ident_f32[:])
            spread_banks[plane] = q_t

        def group_query(plane):
            b, e = divmod(plane, 2)
            nc.scalar.copy(
                out=grouped[:, 0, b * PIXELS : (b + 1) * PIXELS, :].rearrange("p n t -> p (n t)")
                .bitcast(F32)
                .rearrange("p (h e q u) -> p e h q u", h=2, e=2, u=2)[:, e],
                in_=spread_banks[plane][:].rearrange("p u (h q) -> p h q u", h=2),
            )

        def normalise(plane, halves=slice(0, 2)):
            b, e = divmod(plane, 2)
            count = halves.stop - halves.start
            nc.vector.scalar_tensor_tensor(
                out=grouped[:, 0, b * PIXELS : (b + 1) * PIXELS, :].rearrange(
                    "p (h e q) t -> p e h q t", h=2, e=2
                )[:, e, halves],
                in0=spread_banks[plane][:, 0:PAIRS]
                .rearrange("p (h q) -> p h q", h=2)[:, halves]
                .unsqueeze(3)
                .to_broadcast([P, count, QUARTER, PACK]),
                scalar=1.0 / L2_EPS,
                in1=x_sb[:, b].rearrange("p t (h q e) -> p e h q t", h=2, e=2)[:, e, halves],
                op0=ALU.min,
                op1=ALU.mult,
            )

        def transpose_memory(b):
            m_t = psum.tile([P, 2, 2, 2, QUARTER], F32, tag="m_t_then_y", name="m_t%d" % b, bufs=BATCH)
            for e in range(2):
                words = mem_sb[:, b, e, :].bitcast(F32)
                for u in range(2):
                    nc.tensor.transpose(m_t[:, u, :, e, :], words[:, u : CHANNELS // 2 : 2], ident_f32[:])
            mem_banks[b] = m_t

        def group_memory(copy, b):
            copy(
                out=grouped[:, 1, b * PIXELS : (b + 1) * PIXELS, :].rearrange("p n t -> p (n t)")
                .bitcast(F32)
                .rearrange("p (n u) -> p n u", u=2),
                in_=mem_banks[b][:].rearrange("p u h e q -> p (h e q) u"),
            )

        def vector_memory_half(b, h):
            first = b * PIXELS + h * HALF
            nc.vector.tensor_copy(
                out=grouped[:, 1, first : first + HALF, :].rearrange("p n t -> p (n t)")
                .bitcast(F32)
                .rearrange("p (n u) -> p n u", u=2),
                in_=mem_banks[b][:, :, h].rearrange("p u e q -> p (e q) u"),
            )

        def scalar_memory_half(b, h):
            first = b * PIXELS + h * HALF
            nc.scalar.copy(
                out=grouped[:, 1, first : first + HALF, :].rearrange("p n t -> p (n t)")
                .bitcast(F32)
                .rearrange("p (n u) -> p n u", u=2),
                in_=mem_banks[b][:, :, h].rearrange("p u e q -> p (e q) u"),
            )

        def group_memory_quarter(b, h, e):
            first = b * PIXELS + h * HALF + e * QUARTER
            nc.scalar.copy(
                out=grouped[:, 1, first : first + QUARTER, :].rearrange("p n t -> p (n t)")
                .bitcast(F32)
                .rearrange("p (n u) -> p n u", u=2),
                in_=mem_banks[b][:, :, h, e, :].rearrange("p u q -> p q u"),
            )

        def quantise(g, b, halves=slice(0, 2)):
            cols = slice(b * PIXELS + halves.start * HALF, b * PIXELS + halves.stop * HALF)
            nc.vector.quantize_mx(
                out=codes[:, g, cols].bitcast(FP8X4),
                scales=scales[:, g, cols],
                in_=grouped[:, g, cols, :].rearrange("p n t -> p (n t)"),
            )

        def new_bank(tag, b, h):
            return psum.tile([P, PIXELS], F32, tag=tag, name="y_bank%d_%d" % (b, h), bufs=BATCH if tag == "m_t_then_y" else 2)

        def multiply(b, h, g, y, start):
            cols = slice(b * PIXELS + h * HALF, b * PIXELS + (h + 1) * HALF)
            nc.tensor.matmul_mx(
                out=y,
                lhsT=w_words[:, g, :].bitcast(FP4X4),
                lhsT_scale=w_scales[:, g, :],
                rhs=codes[:, g, cols].bitcast(FP8X4),
                rhs_scale=scales[:, g, cols],
                start=start,
                stop=not start,
            )

        def scalar_mean(b, y):
            nc.scalar.activation(
                out=unread[:, b, 0, :],
                in_=y,
                func=ACT.Identity,
                scale=1.0 / PIXELS,
                accum_out=stats[:, 3 * b + 1 : 3 * b + 2],
            )

        def scalar_variance(b, y):
            nc.scalar.activation(
                out=unread[:, b, 1, :],
                in_=y,
                func=ACT.Square,
                scale=-1.0,
                bias=stats[:, 3 * b + 1 : 3 * b + 2],
                accum_out=stats[:, 3 * b + 2 : 3 * b + 3],
            )

        def vector_statistics(b, h, y):
            first = 3 * SCALAR_STATS + 6 * (2 * (b - SCALAR_STATS) + h)
            nc.vector.bn_stats(out=stats[:, first : first + 6], in_=y)

        transpose_query(0)
        sum_squares(0)
        invert_norm(0)
        transpose_memory(0)
        group_memory(nc.vector.tensor_copy, 0)
        quantise(1, 0)
        transpose_query(1)
        spread_norm(0)
        normalise(0)
        sum_squares(1)
        transpose_memory(1)
        group_memory(nc.vector.tensor_copy, 1)
        transpose_query(2)
        sum_squares(2)
        invert_norm(1)
        spread_norm(1)
        normalise(1)
        sum_squares(3)
        invert_norm(2)
        spread_norm(2)
        quantise(1, 1)
        invert_norm(3)
        normalise(2)
        transpose_query(3)
        spread_norm(3)
        sum_squares(4)
        normalise(3)
        quantise(0, 0)
        transpose_memory(2)
        sum_squares(5)
        invert_norm(4)
        spread_norm(4)
        normalise(4)
        quantise(0, 1)
        sum_squares(6)
        guard(5)
        scalar_memory_half(2, 0)
        invert_norm(6)
        invert_guarded(5)
        transpose_memory(3)
        spread_norm(6)
        normalise(6)
        sum_squares(7)
        scalar_memory_half(2, 1)
        invert_norm(7)
        spread_norm(7)
        quantise(1, 2)
        normalise(7)
        y = {}
        y[0] = new_bank("m_t_then_y", 0, 0)
        for h in range(2):
            multiply(0, h, 1, y[0][:, h * HALF : (h + 1) * HALF], True)
            multiply(0, h, 0, y[0][:, h * HALF : (h + 1) * HALF], False)
        scalar_normalise(5)
        transpose_back(5)
        scalar_memory_half(3, 0)
        scalar_memory_half(3, 1)
        scalar_mean(0, y[0][:])
        quantise(1, 3)
        y[1] = new_bank("m_t_then_y", 1, 0)
        for h in range(2):
            multiply(1, h, 1, y[1][:, h * HALF : (h + 1) * HALF], True)
            multiply(1, h, 0, y[1][:, h * HALF : (h + 1) * HALF], False)
        y[2, 0] = new_bank("m_t_then_y", 2, 0)
        multiply(2, 0, 1, y[2, 0][:, 0:HALF], True)
        y[2, 1] = new_bank("m_t_then_y", 2, 1)
        multiply(2, 1, 1, y[2, 1][:, 0:HALF], True)
        y[3, 0] = new_bank("x_t", 3, 0)
        multiply(3, 0, 1, y[3, 0][:, 0:HALF], True)
        group_query(5)
        y[3, 1] = new_bank("x_t", 3, 1)
        multiply(3, 1, 1, y[3, 1][:, 0:HALF], True)
        nc.scalar.copy(out=gamma_and_u[:, 0:1], in_=gamma[:])
        nc.scalar.mul(out=minus_gamma[:], in_=gamma[:], mul=-1.0)
        nc.scalar.copy(out=zero_and_beta[:, 1:2], in_=beta[:])
        quantise(0, 3)
        quantise(0, 2, slice(0, 1))
        quantise(0, 2, slice(1, 2))
        multiply(3, 0, 0, y[3, 0][:, 0:HALF], False)
        multiply(3, 1, 0, y[3, 1][:, 0:HALF], False)
        scalar_mean(1, y[1][:])
        scalar_variance(0, y[0][:])
        scalar_variance(1, y[1][:])
        multiply(2, 0, 0, y[2, 0][:, 0:HALF], False)
        multiply(2, 1, 0, y[2, 1][:, 0:HALF], False)
        vector_statistics(3, 0, y[3, 0][:, 0:HALF])
        vector_statistics(3, 1, y[3, 1][:, 0:HALF])
        vector_statistics(2, 0, y[2, 0][:, 0:HALF])
        vector_statistics(2, 1, y[2, 1][:, 0:HALF])

        mean_var = keep.tile([P, 2], F32)
        nc.vector.bn_aggr(out=mean_var[:], in_=stats[:])
        inv_std = keep.tile([P, 1], F32)
        nc.scalar.activation(out=inv_std[:], in_=mean_var[:, 1:2], func=ACT.Abs_reciprocal_sqrt, bias=BN_EPS)
        nc.vector.tensor_tensor(out=gamma_and_u[:, 1:2], in0=mean_var[:, 0:1], in1=minus_gamma[:], op=ALU.mult)
        scale_shift = keep.tile([P, 2], F32)
        nc.vector.scalar_tensor_tensor(
            out=scale_shift[:],
            in0=gamma_and_u[:],
            scalar=inv_std[:],
            in1=zero_and_beta[:],
            op0=ALU.mult,
            op1=ALU.add,
        )
        scale = scale_shift[:, 0:1]
        shift = scale_shift[:, 1:2]
        result = keep.tile([P, BATCH, PIXELS], F32, align_bytes=256)
        out_view = out.rearrange("b o h w -> b o (h w)")

        def store(b, pixels):
            nc.sync.dma_start(out=out_view[b, :, pixels], in_=result[:, b, pixels])

        def by_pixels(y):
            return y.rearrange("o (h e q) -> o h q e", e=2, q=QUARTER)

        def in_order(b, pixels):
            return result[:, b, pixels].rearrange("o (h q e) -> o h q e", e=2, q=QUARTER)

        def scalar_finish(b, pixels, y):
            nc.scalar.activation(
                out=in_order(b, pixels), in_=by_pixels(y), func=ACT.Relu, bias=shift, scale=scale
            )
            store(b, pixels)

        def vector_affine(b, pixels, y):
            nc.vector.scalar_tensor_tensor(
                out=result[:, b, pixels].rearrange("o (q e) -> o q e", e=2),
                in0=y.rearrange("o (e q) -> o q e", e=2),
                scalar=scale,
                in1=shift.unsqueeze(2).to_broadcast([P, QUARTER, 2]),
                op0=ALU.mult,
                op1=ALU.add,
            )

        def vector_relu(b, pixels):
            nc.vector.tensor_scalar_max(out=result[:, b, pixels], in0=result[:, b, pixels], scalar1=0.0)
            store(b, pixels)

        half = (slice(0, HALF), slice(HALF, PIXELS))
        whole = slice(0, PIXELS)
        scalar_finish(2, half[0], y[2, 0][:, 0:HALF])
        vector_affine(3, half[0], y[3, 0][:, 0:HALF])
        scalar_finish(2, half[1], y[2, 1][:, 0:HALF])
        vector_affine(3, half[1], y[3, 1][:, 0:HALF])
        vector_relu(3, whole)
        scalar_finish(0, whole, y[0][:])
        scalar_finish(1, whole, y[1][:])
